import numpy as np
import ml_dtypes


def mxq(x, axis, fmt="e4m3"):
    dtype, down = {"e4m3": (ml_dtypes.float8_e4m3fn, 7), "e5m2": (ml_dtypes.float8_e5m2, 14)}[fmt]
    v = np.moveaxis(np.asarray(x, np.float32).astype(ml_dtypes.bfloat16).astype(np.float64), axis, -1)
    blocks = v.reshape(v.shape[:-1] + (-1, 32))
    amax = np.abs(blocks).max(-1, keepdims=True)
    byte = np.maximum(np.where(amax > 0, np.frexp(amax)[1] - 1 + 127, 0) - down, 1)
    scale = np.exp2(byte - 127.0)
    codes = (blocks / scale).astype(np.float32).astype(dtype).astype(np.float64)
    return np.moveaxis((codes * scale).reshape(v.shape), -1, axis)


WIDE = False


def mx_kscale(k):
    if not WIDE:
        return np.ones(k)
    levels = np.array([10, -10, 5, -5, 0])
    if k % 512:
        return np.exp2(np.random.permutation(np.resize(levels, k // 32))).repeat(32)
    a = np.empty((k // 512, 16))
    for p in range(k // 512):
        a[p, :8] = np.random.permutation(np.resize(levels, 8))
        for g in range(8):
            far = levels[np.abs(levels - a[p, g]) >= 10]
            a[p, g + 8] = far[np.random.randint(len(far))]
    return np.exp2(a.ravel()).repeat(32)


BF16 = ml_dtypes.bfloat16


def bf(x):
    return np.asarray(x, np.float32).astype(BF16)


def f64(x):
    return np.asarray(x).astype(np.float64)


B, L, S, D, H = 2, 384, 128, 1024, 8
HD = D // H
T = S + L
EPS = 1e-6


def rmsnorm(t, w):
    return t / np.sqrt(np.mean(t * t, axis=-1, keepdims=True) + EPS) * w


def to_mha(t):
    return t.reshape(t.shape[0], t.shape[1], H, HD).transpose(0, 2, 1, 3)


def apply_rope(t, cos, sin):
    tr, ti = t[..., 0::2], t[..., 1::2]
    return np.stack([tr * cos - ti * sin, tr * sin + ti * cos], axis=-1).reshape(t.shape)


def pre_qk(t, Wqk, qn, kn):
    qk = mxq(f64(t), 2, "e4m3") @ mxq(f64(Wqk), 0, "e4m3")
    q, k = qk[..., :D], qk[..., D:]
    return rmsnorm(to_mha(q), f64(qn)), rmsnorm(to_mha(k), f64(kn))


def draw0():
    s = mx_kscale(D)
    inv = 1.0 / (10000.0 ** (np.arange(0, HD, 2) / HD))
    off = np.random.randint(0, T, (B, 1, 1))
    ang = (np.arange(T)[None, :, None] + off) * inv[None, None, :]
    return {
        "x": bf(np.random.standard_normal((B, L, D)) * s),
        "c": bf(np.random.standard_normal((B, S, D)) * s),
        "freqs_cis": bf(np.stack([np.cos(ang), np.sin(ang)], axis=-1)),
        "Wqk_x": bf(np.random.standard_normal((D, 2 * D)) / np.sqrt(D) / s[:, None]),
        "qn_x": bf(1.0 + 0.1 * np.random.standard_normal(HD)),
        "kn_x": bf(1.0 + 0.1 * np.random.standard_normal(HD)),
        "Wqk_c": bf(np.random.standard_normal((D, 2 * D)) / np.sqrt(D) / s[:, None]),
        "qn_c": bf(1.0 + 0.1 * np.random.standard_normal(HD)),
        "kn_c": bf(1.0 + 0.1 * np.random.standard_normal(HD)),
    }


def core(x, c, freqs_cis, Wqk_x, qn_x, kn_x, Wqk_c, qn_c, kn_c):
    qc, kc = pre_qk(c, Wqk_c, qn_c, kn_c)
    qx, kx = pre_qk(x, Wqk_x, qn_x, kn_x)
    q = np.concatenate([qc, qx], axis=2)
    k = np.concatenate([kc, kx], axis=2)
    f = f64(freqs_cis)
    cos = f[..., 0][:, None]
    sin = f[..., 1][:, None]
    return apply_rope(q, cos, sin), apply_rope(k, cos, sin)


def e4m3fn_bytes(y):
    return np.clip(np.asarray(y, np.float64), -448.0, 448.0).astype(np.float32).astype(ml_dtypes.float8_e4m3fn).view(np.uint8)


def e4m3fn_values(b):
    return np.asarray(b, np.uint8).view(ml_dtypes.float8_e4m3fn).astype(np.float64)


def setup_inputs():
    d = draw0()
    x0 = np.asarray(d['Wqk_x']).astype(np.float64)
    s = (np.max(np.abs(x0), axis=(1,), keepdims=True) / 448.0).astype(np.float32)
    out = {}
    for k, v in d.items():
        if k == 'Wqk_x':
            out['Wqk_x_bytes'] = e4m3fn_bytes(x0 / s.astype(np.float64))
            out['Wqk_x_scale'] = s
        else:
            out[k] = v
    return out


def reference(x, c, freqs_cis, Wqk_x_bytes, Wqk_x_scale, qn_x, kn_x, Wqk_c, qn_c, kn_c):
    return core(x, c, freqs_cis, e4m3fn_values(Wqk_x_bytes) * Wqk_x_scale.astype(np.float64), qn_x, kn_x, Wqk_c, qn_c, kn_c)

@@ -1,0 +1,242 @@
+from contextlib import ExitStack
+
+import concourse.mybir as mybir
+from concourse.masks import make_identity
+
+FLOPS = 2 * 1024 * 1024 * 2048
+
+F32 = mybir.dt.float32
+BF16 = mybir.dt.bfloat16
+U32 = mybir.dt.uint32
+U8 = mybir.dt.uint8
+FP8 = mybir.dt.float8_e4m3fn
+FP8X4 = mybir.dt.float8_e4m3fn_x4
+ACT = mybir.ActivationFunctionType
+ALU = mybir.AluOpType
+
+P = 128
+D = 1024
+HD = 128
+CH = 512
+NCH = 4
+EPS = 1e-6
+
+X_INTERLEAVE = {(3, 1): "V"}
+
+
+def tile_dualstreamattentionwithrotaryembedding_pa_kernel(
+    tc, x, c, freqs_cis, Wqk_x_bytes, Wqk_x_scale, qn_x, kn_x, Wqk_c, qn_c, kn_c, out_0, out_1
+):
+    nc = tc.nc
+    outs = (out_0, out_1)
+    with ExitStack() as ctx:
+        keep = ctx.enter_context(tc.tile_pool(name="keep", bufs=1))
+        stage = ctx.enter_context(tc.tile_pool(name="stage", bufs=4))
+        small = ctx.enter_context(tc.tile_pool(name="small", bufs=8))
+        psum = ctx.enter_context(tc.psum_pool(name="psum", bufs=8))
+
+        ident = keep.tile([P, P], F32, name="ident")
+        make_identity(nc, ident[:])
+        one = keep.tile([P, 1], F32, name="one")
+        nc.vector.memset(one[:], 1.0)
+        warm = keep.tile([P, 1], F32, name="warm")
+        nc.scalar.activation(out=warm[:], in_=one[:], func=ACT.Abs_reciprocal_sqrt)
+
+        wc_view = Wqk_c.rearrange("(g p t) n -> g p t n", p=P, t=4)
+        wx_view = Wqk_x_bytes.rearrange("(g p t) n -> g p t n", p=P, t=4)
+        wc_raw = {}
+        wx_bytes = {}
+        tok = {}
+
+        def load_wc(j):
+            for g in range(2):
+                t = keep.tile([P, 4, CH], BF16, name="wc_raw_%d_%d" % (j, g))
+                nc.sync.dma_start(out=t[:], in_=wc_view[g][:, :, j * CH : (j + 1) * CH])
+                wc_raw[(j, g)] = t
+
+        def load_wx(j):
+            for g in range(2):
+                t = keep.tile([P, 4, CH], U8, name="wx_bytes_%d_%d" % (j, g))
+                nc.sync.dma_start(out=t[:], in_=wx_view[g][:, :, j * CH : (j + 1) * CH])
+                wx_bytes[(j, g)] = t
+
+        def load_tok(b, pt):
+            t = keep.tile([P, D], BF16, name="tok_%d_%d" % (b, pt))
+            if pt == 0:
+                nc.sync.dma_start(out=t[:], in_=c[b])
+            else:
+                nc.sync.dma_start(out=t[:], in_=x[b, (pt - 1) * P : pt * P, :])
+            tok[(b, pt)] = t
+
+        load_wc(0)
+        wx_scale = keep.tile([P, 2, 4], F32, name="wx_scale")
+        nc.sync.dma_start(out=wx_scale[:], in_=Wqk_x_scale.rearrange("(g p t) o -> p g (t o)", p=P, t=4))
+        load_wx(0)
+        load_tok(0, 0)
+        load_tok(1, 0)
+        load_wc(1)
+        gw = keep.tile([P, 4, HD], BF16, name="gw")
+        for i, vec in enumerate((qn_c, kn_c, qn_x, kn_x)):
+            nc.sync.dma_start(out=gw[:, i, :], in_=vec.partition_broadcast(P))
+        fr = keep.tile([P, 8, 64, 2], BF16, name="fr")
+        nc.sync.dma_start(
+            out=fr[:].rearrange("p t j c -> p t (j c)"),
+            in_=freqs_cis.rearrange("b (t p) j c -> p (b t) (j c)", p=P),
+        )
+        load_wx(1)
+        load_wc(2)
+        load_wc(3)
+        for b in range(2):
+            for pt in range(1, 4):
+                load_tok(b, pt)
+        load_wx(2)
+        load_wx(3)
+
+        tokc = {}
+        toks = {}
+        wcodes = {}
+        wscales = {}
+        tabA = {}
+        tabB = {}
+
+        def prep_tok(b, pt):
+            words = tok[(b, pt)][:].bitcast(F32)
+            xt = psum.tile([P, 4, P], F32, name="xt", tag="bank")
+            for g in range(2):
+                for u in range(2):
+                    nc.tensor.transpose(xt[:, 2 * g + u, :], words[:, 256 * g + u : 256 * (g + 1) : 2], ident[:])
+            grouped = stage.tile([P, D], BF16, name="tokg", align_bytes=64)
+            nc.scalar.copy(
+                out=grouped[:].bitcast(F32).rearrange("p (g r u) -> p g r u", g=2, u=2),
+                in_=xt[:].rearrange("p (g u) r -> p g r u", g=2),
+            )
+            codes = keep.tile([P, 2 * P], U32, name="tokc_%d_%d" % (b, pt), align_bytes=64)
+            scl = keep.tile([P, 2 * P], U8, name="toks_%d_%d" % (b, pt), align_bytes=64)
+            nc.vector.quantize_mx(out=codes[:].bitcast(FP8X4), scales=scl[:], in_=grouped[:])
+            tokc[(b, pt)] = codes
+            toks[(b, pt)] = scl
+
+        def interleave_quantize(stream, j, g, src, eng):
+            grouped = stage.tile([P, 4 * CH], BF16, name="wg", align_bytes=64)
+            o = grouped[:].rearrange("p (n t) -> p n t", t=4)
+            i = src[:].rearrange("p t n -> p n t")
+            if eng == "V":
+                nc.vector.tensor_copy(out=o, in_=i)
+            else:
+                nc.scalar.copy(out=o, in_=i)
+            codes = keep.tile([P, CH], U32, name="wcod_%s_%d_%d" % (stream, j, g), align_bytes=64)
+            scl = keep.tile([P, CH], U8, name="wscl_%s_%d_%d" % (stream, j, g), align_bytes=64)
+            nc.vector.quantize_mx(out=codes[:].bitcast(FP8X4), scales=scl[:], in_=grouped[:])
+            wcodes[(stream, j, g)] = codes
+            wscales[(stream, j, g)] = scl
+
+        def prep_wc(j):
+            for g in range(2):
+                interleave_quantize("c", j, g, wc_raw[(j, g)], "V")
+
+        def prep_wx(j):
+            for g in range(2):
+                wide = stage.tile([P, 4, CH], BF16, name="wide")
+                for t in range(4):
+                    nc.scalar.activation(
+                        out=wide[:, t, :],
+                        in_=wx_bytes[(j, g)][:, t, :].bitcast(FP8),
+                        func=ACT.Copy,
+                        scale=wx_scale[:, g, t : t + 1],
+                    )
+                interleave_quantize("x", j, g, wide, X_INTERLEAVE.get((j, g), "S"))
+
+        gw4 = gw[:].rearrange("p i (j e) -> p i j e", e=2)
+        gsw = keep.tile([P, 4, 64, 2], BF16, name="gsw")
+
+        def prep_gains():
+            nc.vector.tensor_scalar(
+                out=gsw[:, :, :, 0], in0=gw4[:, :, :, 1], scalar1=-1.0, scalar2=None, op0=ALU.mult
+            )
+            nc.vector.tensor_copy(out=gsw[:, :, :, 1], in_=gw4[:, :, :, 0])
+
+        def build_tables(b, pt):
+            ft = 4 * b + pt
+            s = 0 if pt == 0 else 1
+            cosb = fr[:, ft, :, 0:1].to_broadcast([P, 64, 2])
+            sinb = fr[:, ft, :, 1:2].to_broadcast([P, 64, 2])
+            for qk in range(2):
+                ta = keep.tile([P, 64, 2], F32, name="tabA_%d_%d" % (ft, qk))
+                tb = keep.tile([P, 64, 2], F32, name="tabB_%d_%d" % (ft, qk))
+                nc.vector.tensor_tensor(out=ta[:], in0=gw4[:, 2 * s + qk], in1=cosb, op=ALU.mult)
+                nc.vector.tensor_tensor(out=tb[:], in0=gsw[:, 2 * s + qk], in1=sinb, op=ALU.mult)
+                tabA[(b, pt, qk)] = ta
+                tabB[(b, pt, qk)] = tb
+
+        def bank(stream, b, pt, j):
+            qk = j // 2
+            acc = psum.tile([P, CH], F32, name="acc", tag="bank")
+            for g in range(2):
+                nc.tensor.matmul_mx(
+                    out=acc[:],
+                    lhsT=tokc[(b, pt)][:, g * P : (g + 1) * P].bitcast(FP8X4),
+                    lhsT_scale=toks[(b, pt)][:, g * P : (g + 1) * P],
+                    rhs=wcodes[(stream, j, g)][:].bitcast(FP8X4),
+                    rhs_scale=wscales[(stream, j, g)][:],
+                    start=(g == 0),
+                    stop=(g == 1),
+                )
+            ss = small.tile([P, 4], F32, name="ss")
+            for h in range(4):
+                junk = stage.tile([P, HD], BF16, name="junk")
+                nc.scalar.activation(
+                    out=junk[:], in_=acc[:, h * HD : (h + 1) * HD], func=ACT.Square, accum_out=ss[:, h : h + 1]
+                )
+            rstd = small.tile([P, 4], F32, name="rstd")
+            nc.scalar.activation(out=rstd[:], in_=ss[:], func=ACT.Abs_reciprocal_sqrt, scale=1.0 / HD, bias=EPS)
+            u = stage.tile([P, 4, 64, 2], F32, name="u")
+            v = stage.tile([P, 4, 64, 2], F32, name="v")
+            for h in range(4):
+                th = acc[:, h * HD : (h + 1) * HD].rearrange("p (j e) -> p j e", e=2)
+                nc.vector.scalar_tensor_tensor(
+                    out=u[:, h], in0=th, scalar=rstd[:, h : h + 1], in1=tabA[(b, pt, qk)][:], op0=ALU.mult, op1=ALU.mult
+                )
+                nc.vector.scalar_tensor_tensor(
+                    out=v[:, h],
+                    in0=th[:, :, ::-1],
+                    scalar=rstd[:, h : h + 1],
+                    in1=tabB[(b, pt, qk)][:],
+                    op0=ALU.mult,
+                    op1=ALU.mult,
+                )
+            r = stage.tile([P, 4, HD], F32, name="r")
+            nc.gpsimd.tensor_tensor(
+                out=r[:].rearrange("p h d -> p (h d)"),
+                in0=u[:].rearrange("p h j e -> p (h j e)"),
+                in1=v[:].rearrange("p h j e -> p (h j e)"),
+                op=ALU.add,
+            )
+            h0 = 4 * (j % 2)
+            nc.sync.dma_start(
+                out=outs[qk][b, h0 : h0 + 4, pt * P : (pt + 1) * P, :].rearrange("h p d -> p h d"), in_=r[:]
+            )
+
+        prep_wc(0)
+        prep_tok(0, 0)
+        prep_tok(1, 0)
+        prep_wx(0)
+        prep_wc(1)
+        prep_wc(2)
+        prep_wc(3)
+        prep_gains()
+        build_tables(0, 0)
+        build_tables(1, 0)
+        for j in range(NCH):
+            for b in range(2):
+                bank("c", b, 0, j)
+        for b in range(2):
+            for pt in range(1, 4):
+                prep_tok(b, pt)
+                build_tables(b, pt)
+        prep_wx(1)
+        for j in range(NCH):
+            if j + 2 < NCH:
+                prep_wx(j + 2)
+            for b in range(2):
+                for pt in range(1, 4):
+                    bank("x", b, pt, j)

@@ -21,7 +21,7 @@ CH = 512
 NCH = 4
 EPS = 1e-6
 
-X_INTERLEAVE = {(3, 1): "V"}
+X_METHOD = ("S", "PE", "PE", "PE")
 
 
 def tile_dualstreamattentionwithrotaryembedding_pa_kernel(
@@ -31,14 +31,21 @@ def tile_dualstreamattentionwithrotaryembedding_pa_kernel(
     outs = (out_0, out_1)
     with ExitStack() as ctx:
         keep = ctx.enter_context(tc.tile_pool(name="keep", bufs=1))
-        stage = ctx.enter_context(tc.tile_pool(name="stage", bufs=4))
-        small = ctx.enter_context(tc.tile_pool(name="small", bufs=8))
+        stage = ctx.enter_context(tc.tile_pool(name="stage", bufs=3))
+        small = ctx.enter_context(tc.tile_pool(name="small", bufs=6))
         psum = ctx.enter_context(tc.psum_pool(name="psum", bufs=8))
+        ctx.enter_context(tc.manual_schedule())
 
         ident = keep.tile([P, P], F32, name="ident")
         make_identity(nc, ident[:])
+        ident_bf = keep.tile([P, P], BF16, name="ident_bf")
+        make_identity(nc, ident_bf[:])
+        ones_bf = keep.tile([P, P], BF16, name="ones_bf")
+        nc.gpsimd.memset(ones_bf[:], 1.0)
+        grow = keep.tile([P, 4 * HD], BF16, name="grow")
+        nc.gpsimd.memset(grow[:], 0.0)
         one = keep.tile([P, 1], F32, name="one")
-        nc.vector.memset(one[:], 1.0)
+        nc.gpsimd.memset(one[:], 1.0)
         warm = keep.tile([P, 1], F32, name="warm")
         nc.scalar.activation(out=warm[:], in_=one[:], func=ACT.Abs_reciprocal_sqrt)
 
@@ -47,10 +54,20 @@ def tile_dualstreamattentionwithrotaryembedding_pa_kernel(
         wc_raw = {}
         wx_bytes = {}
         tok = {}
+        tokt = {}
+        tokg = {}
+        tokc = {}
+        toks = {}
+        wgrp = {}
+        wides = {}
+        pbs = {}
+        wcodes = {}
+        wscales = {}
+        tabA = {}
 
-        def load_wc(j):
+        def load_wc(pool, j):
             for g in range(2):
-                t = keep.tile([P, 4, CH], BF16, name="wc_raw_%d_%d" % (j, g))
+                t = pool.tile([P, 4, CH], BF16, name="wc_raw_%d_%d" % (j, g))
                 nc.sync.dma_start(out=t[:], in_=wc_view[g][:, :, j * CH : (j + 1) * CH])
                 wc_raw[(j, g)] = t
 
@@ -60,183 +77,294 @@ def tile_dualstreamattentionwithrotaryembedding_pa_kernel(
                 nc.sync.dma_start(out=t[:], in_=wx_view[g][:, :, j * CH : (j + 1) * CH])
                 wx_bytes[(j, g)] = t
 
-        def load_tok(b, pt):
-            t = keep.tile([P, D], BF16, name="tok_%d_%d" % (b, pt))
+        def load_tok(pool, b, pt):
+            t = pool.tile([P, D], BF16, name="tok_%d_%d" % (b, pt))
             if pt == 0:
                 nc.sync.dma_start(out=t[:], in_=c[b])
             else:
                 nc.sync.dma_start(out=t[:], in_=x[b, (pt - 1) * P : pt * P, :])
             tok[(b, pt)] = t
 
-        load_wc(0)
-        wx_scale = keep.tile([P, 2, 4], F32, name="wx_scale")
-        nc.sync.dma_start(out=wx_scale[:], in_=Wqk_x_scale.rearrange("(g p t) o -> p g (t o)", p=P, t=4))
-        load_wx(0)
-        load_tok(0, 0)
-        load_tok(1, 0)
-        load_wc(1)
-        gw = keep.tile([P, 4, HD], BF16, name="gw")
-        for i, vec in enumerate((qn_c, kn_c, qn_x, kn_x)):
-            nc.sync.dma_start(out=gw[:, i, :], in_=vec.partition_broadcast(P))
-        fr = keep.tile([P, 8, 64, 2], BF16, name="fr")
-        nc.sync.dma_start(
-            out=fr[:].rearrange("p t j c -> p t (j c)"),
-            in_=freqs_cis.rearrange("b (t p) j c -> p (b t) (j c)", p=P),
-        )
-        load_wx(1)
-        load_wc(2)
-        load_wc(3)
-        for b in range(2):
-            for pt in range(1, 4):
-                load_tok(b, pt)
-        load_wx(2)
-        load_wx(3)
-
-        tokc = {}
-        toks = {}
-        wcodes = {}
-        wscales = {}
-        tabA = {}
-        tabB = {}
-
-        def prep_tok(b, pt):
+        def tok_turn(b, pt):
             words = tok[(b, pt)][:].bitcast(F32)
             xt = psum.tile([P, 4, P], F32, name="xt", tag="bank")
             for g in range(2):
                 for u in range(2):
                     nc.tensor.transpose(xt[:, 2 * g + u, :], words[:, 256 * g + u : 256 * (g + 1) : 2], ident[:])
-            grouped = stage.tile([P, D], BF16, name="tokg", align_bytes=64)
+            tokt[(b, pt)] = xt
+
+        def tok_copy(pool, b, pt):
+            grouped = pool.tile([P, D], BF16, name="tokg_%d_%d" % (b, pt), align_bytes=64)
             nc.scalar.copy(
                 out=grouped[:].bitcast(F32).rearrange("p (g r u) -> p g r u", g=2, u=2),
-                in_=xt[:].rearrange("p (g u) r -> p g r u", g=2),
+                in_=tokt[(b, pt)][:].rearrange("p (g u) r -> p g r u", g=2),
             )
+            tokg[(b, pt)] = grouped
+
+        def tok_quant(b, pt):
             codes = keep.tile([P, 2 * P], U32, name="tokc_%d_%d" % (b, pt), align_bytes=64)
             scl = keep.tile([P, 2 * P], U8, name="toks_%d_%d" % (b, pt), align_bytes=64)
-            nc.vector.quantize_mx(out=codes[:].bitcast(FP8X4), scales=scl[:], in_=grouped[:])
+            nc.vector.quantize_mx(out=codes[:].bitcast(FP8X4), scales=scl[:], in_=tokg[(b, pt)][:])
             tokc[(b, pt)] = codes
             toks[(b, pt)] = scl
 
-        def interleave_quantize(stream, j, g, src, eng):
-            grouped = stage.tile([P, 4 * CH], BF16, name="wg", align_bytes=64)
-            o = grouped[:].rearrange("p (n t) -> p n t", t=4)
-            i = src[:].rearrange("p t n -> p n t")
-            if eng == "V":
-                nc.vector.tensor_copy(out=o, in_=i)
-            else:
-                nc.scalar.copy(out=o, in_=i)
-            codes = keep.tile([P, CH], U32, name="wcod_%s_%d_%d" % (stream, j, g), align_bytes=64)
-            scl = keep.tile([P, CH], U8, name="wscl_%s_%d_%d" % (stream, j, g), align_bytes=64)
-            nc.vector.quantize_mx(out=codes[:].bitcast(FP8X4), scales=scl[:], in_=grouped[:])
-            wcodes[(stream, j, g)] = codes
-            wscales[(stream, j, g)] = scl
-
-        def prep_wc(j):
-            for g in range(2):
-                interleave_quantize("c", j, g, wc_raw[(j, g)], "V")
-
-        def prep_wx(j):
-            for g in range(2):
-                wide = stage.tile([P, 4, CH], BF16, name="wide")
-                for t in range(4):
-                    nc.scalar.activation(
-                        out=wide[:, t, :],
-                        in_=wx_bytes[(j, g)][:, t, :].bitcast(FP8),
-                        func=ACT.Copy,
-                        scale=wx_scale[:, g, t : t + 1],
-                    )
-                interleave_quantize("x", j, g, wide, X_INTERLEAVE.get((j, g), "S"))
-
-        gw4 = gw[:].rearrange("p i (j e) -> p i j e", e=2)
-        gsw = keep.tile([P, 4, 64, 2], BF16, name="gsw")
-
-        def prep_gains():
-            nc.vector.tensor_scalar(
-                out=gsw[:, :, :, 0], in0=gw4[:, :, :, 1], scalar1=-1.0, scalar2=None, op0=ALU.mult
+        def w_quant(stream, j):
+            codes = keep.tile([P, 2, CH], U32, name="wcod_%s_%d" % (stream, j), align_bytes=64)
+            scl = keep.tile([P, 2, CH], U8, name="wscl_%s_%d" % (stream, j), align_bytes=64)
+            nc.vector.quantize_mx(
+                out=codes[:].rearrange("p g n -> p (g n)").bitcast(FP8X4),
+                scales=scl[:].rearrange("p g n -> p (g n)"),
+                in_=wgrp[(stream, j)][:].rearrange("p g n t -> p (g n t)"),
             )
-            nc.vector.tensor_copy(out=gsw[:, :, :, 1], in_=gw4[:, :, :, 0])
+            wcodes[(stream, j)] = codes
+            wscales[(stream, j)] = scl
+
+        def wc_interleave(j, g):
+            nc.vector.tensor_copy(out=wgrp[("c", j)][:, g], in_=wc_raw[(j, g)][:].rearrange("p t n -> p n t"))
+
+        def wx_widen(j, g, t0, t1):
+            if t0 == 0:
+                wides[(j, g)] = stage.tile([P, 4, CH], BF16, name="wide")
+            for t in range(t0, t1):
+                nc.scalar.activation(
+                    out=wides[(j, g)][:, t, :],
+                    in_=wx_bytes[(j, g)][:, t, :].bitcast(FP8),
+                    func=ACT.Copy,
+                    scale=wx_scale[:, g, t : t + 1],
+                )
+
+        def wx_group(j):
+            wgrp[("x", j)] = stage.tile([P, 2, CH, 4], BF16, name="wgx", bufs=2, align_bytes=64)
+
+        def wx_strided(j, g):
+            nc.scalar.copy(out=wgrp[("x", j)][:, g], in_=wides[(j, g)][:].rearrange("p t n -> p n t"))
+
+        def wx_permute(j, g):
+            for hb in range(2):
+                pb = psum.tile([P, 2 * P, 4], BF16, name="pb", tag="bank")
+                for q in range(2):
+                    n0 = (2 * hb + q) * P
+                    nc.tensor.matmul(
+                        out=pb[:, q * P : (q + 1) * P, :],
+                        lhsT=ident_bf[:],
+                        rhs=wides[(j, g)][:, :, n0 : n0 + P].rearrange("p t n -> p n t"),
+                        start=True,
+                        stop=True,
+                    )
+                pbs[(j, g, hb)] = pb
+
+        def wx_empty(j, g):
+            for hb in range(2):
+                nc.scalar.copy(out=wgrp[("x", j)][:, g, 2 * hb * P : 2 * (hb + 1) * P, :], in_=pbs[(j, g, hb)][:])
+
+        g2 = keep.tile([P, 4, 2, 64, 2], F32, name="g2")
+        pgs = {}
+
+        def gains_spread():
+            pg = psum.tile([P, 4, 64, 2], F32, name="pg", tag="bank")
+            nc.tensor.matmul(
+                out=pg[:].rearrange("p i j e -> p (i j e)"), lhsT=ones_bf[:], rhs=grow[:], start=True, stop=True
+            )
+            pgs[0] = pg
+
+        def gains_copy():
+            pg = pgs[0]
+            nc.vector.tensor_copy(out=g2[:, :, 0], in_=pg[:])
+            nc.vector.tensor_copy(out=g2[:, :, 1, :, 0], in_=pg[:, :, :, 0])
+            nc.vector.tensor_scalar(
+                out=g2[:, :, 1, :, 1], in0=pg[:, :, :, 1], scalar1=-1.0, scalar2=None, op0=ALU.mult
+            )
 
         def build_tables(b, pt):
             ft = 4 * b + pt
             s = 0 if pt == 0 else 1
-            cosb = fr[:, ft, :, 0:1].to_broadcast([P, 64, 2])
-            sinb = fr[:, ft, :, 1:2].to_broadcast([P, 64, 2])
+            cs = fr[:, ft].rearrange("p j c o -> p c j o").to_broadcast([P, 2, 64, 2])
             for qk in range(2):
-                ta = keep.tile([P, 64, 2], F32, name="tabA_%d_%d" % (ft, qk))
-                tb = keep.tile([P, 64, 2], F32, name="tabB_%d_%d" % (ft, qk))
-                nc.vector.tensor_tensor(out=ta[:], in0=gw4[:, 2 * s + qk], in1=cosb, op=ALU.mult)
-                nc.vector.tensor_tensor(out=tb[:], in0=gsw[:, 2 * s + qk], in1=sinb, op=ALU.mult)
+                ta = keep.tile([P, 2, 64, 2], F32, name="tab_%d_%d" % (ft, qk))
+                nc.vector.tensor_tensor(out=ta[:], in0=g2[:, 2 * s + qk], in1=cs, op=ALU.mult)
                 tabA[(b, pt, qk)] = ta
-                tabB[(b, pt, qk)] = tb
 
-        def bank(stream, b, pt, j):
-            qk = j // 2
-            acc = psum.tile([P, CH], F32, name="acc", tag="bank")
-            for g in range(2):
-                nc.tensor.matmul_mx(
-                    out=acc[:],
-                    lhsT=tokc[(b, pt)][:, g * P : (g + 1) * P].bitcast(FP8X4),
-                    lhsT_scale=toks[(b, pt)][:, g * P : (g + 1) * P],
-                    rhs=wcodes[(stream, j, g)][:].bitcast(FP8X4),
-                    rhs_scale=wscales[(stream, j, g)][:],
-                    start=(g == 0),
-                    stop=(g == 1),
-                )
-            ss = small.tile([P, 4], F32, name="ss")
-            for h in range(4):
-                junk = stage.tile([P, HD], BF16, name="junk")
-                nc.scalar.activation(
-                    out=junk[:], in_=acc[:, h * HD : (h + 1) * HD], func=ACT.Square, accum_out=ss[:, h : h + 1]
-                )
-            rstd = small.tile([P, 4], F32, name="rstd")
+        pairs = []
+        for j in range(NCH):
+            pairs.append(("c", j, ((0, 0), (1, 0))))
+        for j in range(NCH):
+            pairs.append(("x", j, ((0, 1), (0, 2))))
+            pairs.append(("x", j, ((0, 3), (1, 1))))
+            pairs.append(("x", j, ((1, 2), (1, 3))))
+        NP = len(pairs)
+        accs = {}
+        rstds = {}
+
+        def mm(i):
+            stream, j, tiles = pairs[i]
+            banks = []
+            for b, pt in tiles:
+                acc = psum.tile([P, CH], F32, name="acc", tag="bank")
+                for g in range(2):
+                    nc.tensor.matmul_mx(
+                        out=acc[:],
+                        lhsT=tokc[(b, pt)][:, g * P : (g + 1) * P].bitcast(FP8X4),
+                        lhsT_scale=toks[(b, pt)][:, g * P : (g + 1) * P],
+                        rhs=wcodes[(stream, j)][:, g, :].bitcast(FP8X4),
+                        rhs_scale=wscales[(stream, j)][:, g, :],
+                        start=(g == 0),
+                        stop=(g == 1),
+                    )
+                banks.append(acc)
+            accs[i] = banks
+
+        def sq(i):
+            ss = small.tile([P, 8], F32, name="ss")
+            for k in range(2):
+                for h in range(4):
+                    junk = small.tile([P, HD], BF16, name="junk")
+                    nc.scalar.activation(
+                        out=junk[:],
+                        in_=accs[i][k][:, h * HD : (h + 1) * HD],
+                        func=ACT.Square,
+                        accum_out=ss[:, 4 * k + h : 4 * k + h + 1],
+                    )
+            rstd = small.tile([P, 8], F32, name="rstd")
             nc.scalar.activation(out=rstd[:], in_=ss[:], func=ACT.Abs_reciprocal_sqrt, scale=1.0 / HD, bias=EPS)
-            u = stage.tile([P, 4, 64, 2], F32, name="u")
-            v = stage.tile([P, 4, 64, 2], F32, name="v")
-            for h in range(4):
-                th = acc[:, h * HD : (h + 1) * HD].rearrange("p (j e) -> p j e", e=2)
-                nc.vector.scalar_tensor_tensor(
-                    out=u[:, h], in0=th, scalar=rstd[:, h : h + 1], in1=tabA[(b, pt, qk)][:], op0=ALU.mult, op1=ALU.mult
-                )
-                nc.vector.scalar_tensor_tensor(
-                    out=v[:, h],
-                    in0=th[:, :, ::-1],
-                    scalar=rstd[:, h : h + 1],
-                    in1=tabB[(b, pt, qk)][:],
-                    op0=ALU.mult,
-                    op1=ALU.mult,
-                )
-            r = stage.tile([P, 4, HD], F32, name="r")
-            nc.gpsimd.tensor_tensor(
-                out=r[:].rearrange("p h d -> p (h d)"),
-                in0=u[:].rearrange("p h j e -> p (h j e)"),
-                in1=v[:].rearrange("p h j e -> p (h j e)"),
-                op=ALU.add,
-            )
-            h0 = 4 * (j % 2)
-            nc.sync.dma_start(
-                out=outs[qk][b, h0 : h0 + 4, pt * P : (pt + 1) * P, :].rearrange("h p d -> p h d"), in_=r[:]
-            )
+            rstds[i] = rstd
 
-        prep_wc(0)
-        prep_tok(0, 0)
-        prep_tok(1, 0)
-        prep_wx(0)
-        prep_wc(1)
-        prep_wc(2)
-        prep_wc(3)
-        prep_gains()
-        build_tables(0, 0)
-        build_tables(1, 0)
-        for j in range(NCH):
-            for b in range(2):
-                bank("c", b, 0, j)
-        for b in range(2):
-            for pt in range(1, 4):
-                prep_tok(b, pt)
+        def rot(rotp, i):
+            stream, j, tiles = pairs[i]
+            qk = j // 2
+            h0 = 4 * (j % 2)
+            uv = rotp.tile([P, 8, 2, HD], F32, name="uv")
+            r = rotp.tile([P, 8, 64, 2], F32, name="r")
+            for k in range(2):
+                b, pt = tiles[k]
+                for h in range(4):
+                    nc.vector.scalar_tensor_tensor(
+                        out=uv[:, 4 * k + h],
+                        in0=accs[i][k][:, h * HD : (h + 1) * HD].rearrange("p (o d) -> p o d", o=1).to_broadcast([P, 2, HD]),
+                        scalar=rstds[i][:, 4 * k + h : 4 * k + h + 1],
+                        in1=tabA[(b, pt, qk)][:].rearrange("p r j e -> p r (j e)"),
+                        op0=ALU.mult,
+                        op1=ALU.mult,
+                    )
+            uv5 = uv[:].rearrange("p h r (j e) -> p h r j e", e=2)
+            if i < NP - 1:
+                nc.gpsimd.tensor_tensor(out=r[:], in0=uv5[:, :, 0], in1=uv5[:, :, 1, :, ::-1], op=ALU.add)
+            for k in range(2):
+                b, pt = tiles[k]
+                hs = slice(4 * k, 4 * k + 4)
+                if i == NP - 1:
+                    nc.vector.tensor_tensor(
+                        out=r[:, hs], in0=uv5[:, hs, 0], in1=uv5[:, hs, 1, :, ::-1], op=ALU.add
+                    )
+                nc.sync.dma_start(
+                    out=outs[qk][b, h0 : h0 + 4, pt * P : (pt + 1) * P, :].rearrange("h p d -> p h d"),
+                    in_=r[:, hs].rearrange("p h j e -> p h (j e)"),
+                )
+
+        XT = [(b, pt) for b in range(2) for pt in range(1, 4)]
+
+        with tc.tile_pool(name="early", bufs=1) as early:
+            wx_scale = keep.tile([P, 2, 4], F32, name="wx_scale")
+            nc.sync.dma_start(out=wx_scale[:], in_=Wqk_x_scale.rearrange("(g p t) o -> p g (t o)", p=P, t=4))
+            load_wc(early, 0)
+            load_wx(0)
+            load_wc(early, 1)
+            load_tok(early, 0, 0)
+            load_tok(early, 1, 0)
+            load_wc(early, 2)
+            load_wx(1)
+            load_wc(early, 3)
+            for i, vec in enumerate((qn_c, kn_c, qn_x, kn_x)):
+                nc.sync.dma_start(out=grow[0:1, i * HD : (i + 1) * HD], in_=vec.rearrange("(o d) -> o d", o=1))
+            fr = keep.tile([P, 8, 64, 2, 1], BF16, name="fr")
+            nc.sync.dma_start(
+                out=fr[:].rearrange("p t j c o -> p t (j c o)"),
+                in_=freqs_cis.rearrange("b (t p) j c -> p (b t) (j c)", p=P),
+            )
+            for b, pt in XT:
+                load_tok(early, b, pt)
+            load_wx(2)
+            load_wx(3)
+
+            def wgc(j):
+                wgrp[("c", j)] = early.tile([P, 2, CH, 4], BF16, name="wgc", bufs=2, align_bytes=64)
+
+            wgc(0)
+            wc_interleave(0, 0)
+            wc_interleave(0, 1)
+            wx_group(0)
+            wx_widen(0, 0, 0, 4)
+            wx_widen(0, 1, 0, 4)
+            wx_strided(0, 0)
+            wx_strided(0, 1)
+            wgc(1)
+            wc_interleave(1, 0)
+            w_quant("c", 0)
+            wc_interleave(1, 1)
+            tok_turn(0, 0)
+            tok_turn(1, 0)
+            tok_copy(early, 0, 0)
+            tok_copy(early, 1, 0)
+            for j in range(2, NCH):
+                wgc(j)
+                wc_interleave(j, 0)
+                w_quant("c", j - 1)
+                wc_interleave(j, 1)
+            gains_spread()
+            wx_group(1)
+            wx_widen(1, 0, 0, 4)
+            wx_permute(1, 0)
+            wx_widen(1, 1, 0, 4)
+            wx_permute(1, 1)
+            wx_empty(1, 0)
+            wx_empty(1, 1)
+            tok_quant(0, 0)
+            tok_quant(1, 0)
+            w_quant("c", NCH - 1)
+            gains_copy()
+            build_tables(0, 0)
+            build_tables(1, 0)
+            for b, pt in XT:
+                tok_turn(b, pt)
+                tok_copy(early, b, pt)
+            w_quant("x", 0)
+            for b, pt in XT:
                 build_tables(b, pt)
-        prep_wx(1)
-        for j in range(NCH):
-            if j + 2 < NCH:
-                prep_wx(j + 2)
-            for b in range(2):
-                for pt in range(1, 4):
-                    bank("x", b, pt, j)
+            w_quant("x", 1)
+            for b, pt in XT:
+                tok_quant(b, pt)
+
+        def late_step(k):
+            j = 2 + k // 6
+            s = k % 6
+            if s == 0:
+                wx_widen(j, 0, 0, 2)
+            elif s == 1:
+                wx_widen(j, 0, 2, 4)
+                wx_permute(j, 0)
+            elif s == 2:
+                wx_widen(j, 1, 0, 2)
+            elif s == 3:
+                wx_group(j)
+                wx_empty(j, 0)
+            elif s == 4:
+                wx_widen(j, 1, 2, 4)
+                wx_permute(j, 1)
+            else:
+                wx_empty(j, 1)
+
+        with tc.tile_pool(name="rotp", bufs=4) as rotp:
+            mm(0)
+            mm(1)
+            sq(0)
+            late_step(0)
+            for i in range(NP):
+                if i + 2 < NP:
+                    nstream, nj, ntiles = pairs[i + 2]
+                    if nstream == "x" and nj >= 2 and ntiles[0] == (0, 1):
+                        w_quant("x", nj)
+                    mm(i + 2)
+                if i + 1 < NP:
+                    sq(i + 1)
+                if i + 1 < 12:
+                    late_step(i + 1)
+                rot(rotp, i)

@@ -228,33 +228,39 @@ def tile_dualstreamattentionwithrotaryembedding_pa_kernel(
             nc.scalar.activation(out=rstd[:], in_=ss[:], func=ACT.Abs_reciprocal_sqrt, scale=1.0 / HD, bias=EPS)
             rstds[i] = rstd
 
-        def rot(rotp, i):
+        uvs = {}
+
+        def rot(rotp, i, first, last):
+            stream, j, tiles = pairs[i]
+            qk = j // 2
+            if first == 0:
+                uvs[i] = rotp.tile([P, 8, 2, HD], F32, name="uv")
+            for hh in range(first, last):
+                k = hh // 4
+                h = hh % 4
+                b, pt = tiles[k]
+                nc.vector.scalar_tensor_tensor(
+                    out=uvs[i][:, hh],
+                    in0=accs[i][k][:, h * HD : (h + 1) * HD].rearrange("p (o d) -> p o d", o=1).to_broadcast([P, 2, HD]),
+                    scalar=rstds[i][:, hh : hh + 1],
+                    in1=tabA[(b, pt, qk)][:].rearrange("p r j e -> p r (j e)"),
+                    op0=ALU.mult,
+                    op1=ALU.mult,
+                )
+
+        def add_store(rotp, i, eng, split):
             stream, j, tiles = pairs[i]
             qk = j // 2
             h0 = 4 * (j % 2)
-            uv = rotp.tile([P, 8, 2, HD], F32, name="uv")
             r = rotp.tile([P, 8, 64, 2], F32, name="r")
-            for k in range(2):
-                b, pt = tiles[k]
-                for h in range(4):
-                    nc.vector.scalar_tensor_tensor(
-                        out=uv[:, 4 * k + h],
-                        in0=accs[i][k][:, h * HD : (h + 1) * HD].rearrange("p (o d) -> p o d", o=1).to_broadcast([P, 2, HD]),
-                        scalar=rstds[i][:, 4 * k + h : 4 * k + h + 1],
-                        in1=tabA[(b, pt, qk)][:].rearrange("p r j e -> p r (j e)"),
-                        op0=ALU.mult,
-                        op1=ALU.mult,
-                    )
-            uv5 = uv[:].rearrange("p h r (j e) -> p h r j e", e=2)
-            if i < NP - 1:
-                nc.gpsimd.tensor_tensor(out=r[:], in0=uv5[:, :, 0], in1=uv5[:, :, 1, :, ::-1], op=ALU.add)
+            uv5 = uvs[i][:].rearrange("p h r (j e) -> p h r j e", e=2)
+            if not split:
+                eng.tensor_tensor(out=r[:], in0=uv5[:, :, 0], in1=uv5[:, :, 1, :, ::-1], op=ALU.add)
             for k in range(2):
                 b, pt = tiles[k]
                 hs = slice(4 * k, 4 * k + 4)
-                if i == NP - 1:
-                    nc.vector.tensor_tensor(
-                        out=r[:, hs], in0=uv5[:, hs, 0], in1=uv5[:, hs, 1, :, ::-1], op=ALU.add
-                    )
+                if split:
+                    eng.tensor_tensor(out=r[:, hs], in0=uv5[:, hs, 0], in1=uv5[:, hs, 1, :, ::-1], op=ALU.add)
                 nc.sync.dma_start(
                     out=outs[qk][b, h0 : h0 + 4, pt * P : (pt + 1) * P, :].rearrange("h p d -> p h d"),
                     in_=r[:, hs].rearrange("p h j e -> p h (j e)"),
@@ -352,19 +358,38 @@ def tile_dualstreamattentionwithrotaryembedding_pa_kernel(
             else:
                 wx_empty(j, 1)
 
+        ON_POOL = (0, 1, 3, 4, 6, 7, 9, 10, 12, 13)
+        STEPS = (2, 1, 1, 2, 1, 1, 2, 1, 1, 0, 0, 0, 0, 0, 0, 0, 0)
         with tc.tile_pool(name="rotp", bufs=4) as rotp:
             mm(0)
             mm(1)
             sq(0)
-            late_step(0)
+            done = 0
+            for k in range(STEPS[0]):
+                late_step(done)
+                done += 1
+            waiting = []
+            quant_at = {6: 2, 9: 3}
             for i in range(NP):
                 if i + 2 < NP:
-                    nstream, nj, ntiles = pairs[i + 2]
-                    if nstream == "x" and nj >= 2 and ntiles[0] == (0, 1):
-                        w_quant("x", nj)
                     mm(i + 2)
                 if i + 1 < NP:
                     sq(i + 1)
-                if i + 1 < 12:
-                    late_step(i + 1)
-                rot(rotp, i)
+                for k in range(STEPS[i + 1]):
+                    late_step(done)
+                    done += 1
+                if i in ON_POOL:
+                    rot(rotp, i, 0, 7)
+                    for w in waiting:
+                        add_store(rotp, w, nc.vector, False)
+                    waiting = []
+                    if i in quant_at:
+                        w_quant("x", quant_at[i])
+                    rot(rotp, i, 7, 8)
+                    add_store(rotp, i, nc.gpsimd, False)
+                else:
+                    rot(rotp, i, 0, 8)
+                    waiting.append(i)
+            for w in waiting[:-1]:
+                add_store(rotp, w, nc.vector, False)
+            add_store(rotp, waiting[-1], nc.vector, True)

@@ -21,7 +21,7 @@ CH = 512
 NCH = 4
 EPS = 1e-6
 
-X_METHOD = ("S", "PE", "PE", "PE")
+X_INTERLEAVE = {(3, 0): "V", (3, 1): "V"}
 
 
 def tile_dualstreamattentionwithrotaryembedding_pa_kernel(
@@ -31,21 +31,14 @@ def tile_dualstreamattentionwithrotaryembedding_pa_kernel(
     outs = (out_0, out_1)
     with ExitStack() as ctx:
         keep = ctx.enter_context(tc.tile_pool(name="keep", bufs=1))
-        stage = ctx.enter_context(tc.tile_pool(name="stage", bufs=3))
-        small = ctx.enter_context(tc.tile_pool(name="small", bufs=6))
+        stage = ctx.enter_context(tc.tile_pool(name="stage", bufs=4))
+        small = ctx.enter_context(tc.tile_pool(name="small", bufs=8))
         psum = ctx.enter_context(tc.psum_pool(name="psum", bufs=8))
-        ctx.enter_context(tc.manual_schedule())
 
         ident = keep.tile([P, P], F32, name="ident")
         make_identity(nc, ident[:])
-        ident_bf = keep.tile([P, P], BF16, name="ident_bf")
-        make_identity(nc, ident_bf[:])
-        ones_bf = keep.tile([P, P], BF16, name="ones_bf")
-        nc.gpsimd.memset(ones_bf[:], 1.0)
-        grow = keep.tile([P, 4 * HD], BF16, name="grow")
-        nc.gpsimd.memset(grow[:], 0.0)
         one = keep.tile([P, 1], F32, name="one")
-        nc.gpsimd.memset(one[:], 1.0)
+        nc.vector.memset(one[:], 1.0)
         warm = keep.tile([P, 1], F32, name="warm")
         nc.scalar.activation(out=warm[:], in_=one[:], func=ACT.Abs_reciprocal_sqrt)
 
@@ -54,20 +47,10 @@ def tile_dualstreamattentionwithrotaryembedding_pa_kernel(
         wc_raw = {}
         wx_bytes = {}
         tok = {}
-        tokt = {}
-        tokg = {}
-        tokc = {}
-        toks = {}
-        wgrp = {}
-        wides = {}
-        pbs = {}
-        wcodes = {}
-        wscales = {}
-        tabA = {}
 
-        def load_wc(pool, j):
+        def load_wc(j):
             for g in range(2):
-                t = pool.tile([P, 4, CH], BF16, name="wc_raw_%d_%d" % (j, g))
+                t = keep.tile([P, 4, CH], BF16, name="wc_raw_%d_%d" % (j, g))
                 nc.sync.dma_start(out=t[:], in_=wc_view[g][:, :, j * CH : (j + 1) * CH])
                 wc_raw[(j, g)] = t
 
@@ -77,102 +60,98 @@ def tile_dualstreamattentionwithrotaryembedding_pa_kernel(
                 nc.sync.dma_start(out=t[:], in_=wx_view[g][:, :, j * CH : (j + 1) * CH])
                 wx_bytes[(j, g)] = t
 
-        def load_tok(pool, b, pt):
-            t = pool.tile([P, D], BF16, name="tok_%d_%d" % (b, pt))
+        def load_tok(b, pt):
+            t = keep.tile([P, D], BF16, name="tok_%d_%d" % (b, pt))
             if pt == 0:
                 nc.sync.dma_start(out=t[:], in_=c[b])
             else:
                 nc.sync.dma_start(out=t[:], in_=x[b, (pt - 1) * P : pt * P, :])
             tok[(b, pt)] = t
 
-        def tok_turn(b, pt):
+        load_wc(0)
+        wx_scale = keep.tile([P, 2, 4], F32, name="wx_scale")
+        nc.sync.dma_start(out=wx_scale[:], in_=Wqk_x_scale.rearrange("(g p t) o -> p g (t o)", p=P, t=4))
+        load_wx(0)
+        load_tok(0, 0)
+        load_tok(1, 0)
+        load_wc(1)
+        gw = keep.tile([P, 4, 64, 2], BF16, name="gw")
+        for i, vec in enumerate((qn_c, kn_c, qn_x, kn_x)):
+            nc.sync.dma_start(out=gw[:, i].rearrange("p j e -> p (j e)"), in_=vec.partition_broadcast(P))
+        fr = keep.tile([P, 8, 64, 2, 1], BF16, name="fr")
+        nc.sync.dma_start(
+            out=fr[:].rearrange("p t j c o -> p t (j c o)"),
+            in_=freqs_cis.rearrange("b (t p) j c -> p (b t) (j c)", p=P),
+        )
+        load_wx(1)
+        load_wc(2)
+        load_wc(3)
+        for b in range(2):
+            for pt in range(1, 4):
+                load_tok(b, pt)
+        load_wx(2)
+        load_wx(3)
+
+        tokc = {}
+        toks = {}
+        wcodes = {}
+        wscales = {}
+        tabA = {}
+
+        def prep_tok(b, pt):
             words = tok[(b, pt)][:].bitcast(F32)
             xt = psum.tile([P, 4, P], F32, name="xt", tag="bank")
             for g in range(2):
                 for u in range(2):
                     nc.tensor.transpose(xt[:, 2 * g + u, :], words[:, 256 * g + u : 256 * (g + 1) : 2], ident[:])
-            tokt[(b, pt)] = xt
-
-        def tok_copy(pool, b, pt):
-            grouped = pool.tile([P, D], BF16, name="tokg_%d_%d" % (b, pt), align_bytes=64)
+            grouped = stage.tile([P, D], BF16, name="tokg", align_bytes=64)
             nc.scalar.copy(
                 out=grouped[:].bitcast(F32).rearrange("p (g r u) -> p g r u", g=2, u=2),
-                in_=tokt[(b, pt)][:].rearrange("p (g u) r -> p g r u", g=2),
+                in_=xt[:].rearrange("p (g u) r -> p g r u", g=2),
             )
-            tokg[(b, pt)] = grouped
-
-        def tok_quant(b, pt):
             codes = keep.tile([P, 2 * P], U32, name="tokc_%d_%d" % (b, pt), align_bytes=64)
             scl = keep.tile([P, 2 * P], U8, name="toks_%d_%d" % (b, pt), align_bytes=64)
-            nc.vector.quantize_mx(out=codes[:].bitcast(FP8X4), scales=scl[:], in_=tokg[(b, pt)][:])
+            nc.vector.quantize_mx(out=codes[:].bitcast(FP8X4), scales=scl[:], in_=grouped[:])
             tokc[(b, pt)] = codes
             toks[(b, pt)] = scl
 
-        def w_quant(stream, j):
-            codes = keep.tile([P, 2, CH], U32, name="wcod_%s_%d" % (stream, j), align_bytes=64)
-            scl = keep.tile([P, 2, CH], U8, name="wscl_%s_%d" % (stream, j), align_bytes=64)
-            nc.vector.quantize_mx(
-                out=codes[:].rearrange("p g n -> p (g n)").bitcast(FP8X4),
-                scales=scl[:].rearrange("p g n -> p (g n)"),
-                in_=wgrp[(stream, j)][:].rearrange("p g n t -> p (g n t)"),
-            )
-            wcodes[(stream, j)] = codes
-            wscales[(stream, j)] = scl
+        def interleave_quantize(stream, j, g, src, eng):
+            grouped = stage.tile([P, 4 * CH], BF16, name="wg", align_bytes=64)
+            o = grouped[:].rearrange("p (n t) -> p n t", t=4)
+            i = src[:].rearrange("p t n -> p n t")
+            if eng == "V":
+                nc.vector.tensor_copy(out=o, in_=i)
+            else:
+                nc.scalar.copy(out=o, in_=i)
+            codes = keep.tile([P, CH], U32, name="wcod_%s_%d_%d" % (stream, j, g), align_bytes=64)
+            scl = keep.tile([P, CH], U8, name="wscl_%s_%d_%d" % (stream, j, g), align_bytes=64)
+            nc.vector.quantize_mx(out=codes[:].bitcast(FP8X4), scales=scl[:], in_=grouped[:])
+            wcodes[(stream, j, g)] = codes
+            wscales[(stream, j, g)] = scl
 
-        def wc_interleave(j, g):
-            nc.vector.tensor_copy(out=wgrp[("c", j)][:, g], in_=wc_raw[(j, g)][:].rearrange("p t n -> p n t"))
+        def prep_wc(j):
+            for g in range(2):
+                interleave_quantize("c", j, g, wc_raw[(j, g)], "V")
 
-        def wx_widen(j, g, t0, t1):
-            if t0 == 0:
-                wides[(j, g)] = stage.tile([P, 4, CH], BF16, name="wide")
-            for t in range(t0, t1):
-                nc.scalar.activation(
-                    out=wides[(j, g)][:, t, :],
-                    in_=wx_bytes[(j, g)][:, t, :].bitcast(FP8),
-                    func=ACT.Copy,
-                    scale=wx_scale[:, g, t : t + 1],
-                )
-
-        def wx_group(j):
-            wgrp[("x", j)] = stage.tile([P, 2, CH, 4], BF16, name="wgx", bufs=2, align_bytes=64)
-
-        def wx_strided(j, g):
-            nc.scalar.copy(out=wgrp[("x", j)][:, g], in_=wides[(j, g)][:].rearrange("p t n -> p n t"))
-
-        def wx_permute(j, g):
-            for hb in range(2):
-                pb = psum.tile([P, 2 * P, 4], BF16, name="pb", tag="bank")
-                for q in range(2):
-                    n0 = (2 * hb + q) * P
-                    nc.tensor.matmul(
-                        out=pb[:, q * P : (q + 1) * P, :],
-                        lhsT=ident_bf[:],
-                        rhs=wides[(j, g)][:, :, n0 : n0 + P].rearrange("p t n -> p n t"),
-                        start=True,
-                        stop=True,
+        def prep_wx(j):
+            for g in range(2):
+                wide = stage.tile([P, 4, CH], BF16, name="wide")
+                for t in range(4):
+                    nc.scalar.activation(
+                        out=wide[:, t, :],
+                        in_=wx_bytes[(j, g)][:, t, :].bitcast(FP8),
+                        func=ACT.Copy,
+                        scale=wx_scale[:, g, t : t + 1],
                     )
-                pbs[(j, g, hb)] = pb
-
-        def wx_empty(j, g):
-            for hb in range(2):
-                nc.scalar.copy(out=wgrp[("x", j)][:, g, 2 * hb * P : 2 * (hb + 1) * P, :], in_=pbs[(j, g, hb)][:])
+                interleave_quantize("x", j, g, wide, X_INTERLEAVE.get((j, g), "S"))
 
         g2 = keep.tile([P, 4, 2, 64, 2], F32, name="g2")
-        pgs = {}
 
-        def gains_spread():
-            pg = psum.tile([P, 4, 64, 2], F32, name="pg", tag="bank")
-            nc.tensor.matmul(
-                out=pg[:].rearrange("p i j e -> p (i j e)"), lhsT=ones_bf[:], rhs=grow[:], start=True, stop=True
-            )
-            pgs[0] = pg
-
-        def gains_copy():
-            pg = pgs[0]
-            nc.vector.tensor_copy(out=g2[:, :, 0], in_=pg[:])
-            nc.vector.tensor_copy(out=g2[:, :, 1, :, 0], in_=pg[:, :, :, 0])
+        def prep_gains():
+            nc.vector.tensor_copy(out=g2[:, :, 0], in_=gw[:])
+            nc.vector.tensor_copy(out=g2[:, :, 1, :, 0], in_=gw[:, :, :, 0])
             nc.vector.tensor_scalar(
-                out=g2[:, :, 1, :, 1], in0=pg[:, :, :, 1], scalar1=-1.0, scalar2=None, op0=ALU.mult
+                out=g2[:, :, 1, :, 1], in0=gw[:, :, :, 1], scalar1=-1.0, scalar2=None, op0=ALU.mult
             )
 
         def build_tables(b, pt):
@@ -184,20 +163,10 @@ def tile_dualstreamattentionwithrotaryembedding_pa_kernel(
                 nc.vector.tensor_tensor(out=ta[:], in0=g2[:, 2 * s + qk], in1=cs, op=ALU.mult)
                 tabA[(b, pt, qk)] = ta
 
-        pairs = []
-        for j in range(NCH):
-            pairs.append(("c", j, ((0, 0), (1, 0))))
-        for j in range(NCH):
-            pairs.append(("x", j, ((0, 1), (0, 2))))
-            pairs.append(("x", j, ((0, 3), (1, 1))))
-            pairs.append(("x", j, ((1, 2), (1, 3))))
-        NP = len(pairs)
-        accs = {}
-        rstds = {}
-
-        def mm(i):
-            stream, j, tiles = pairs[i]
-            banks = []
+        def pair(stream, tiles, j, own=False):
+            qk = j // 2
+            h0 = 4 * (j % 2)
+            accs = []
             for b, pt in tiles:
                 acc = psum.tile([P, CH], F32, name="acc", tag="bank")
                 for g in range(2):
@@ -205,191 +174,69 @@ def tile_dualstreamattentionwithrotaryembedding_pa_kernel(
                         out=acc[:],
                         lhsT=tokc[(b, pt)][:, g * P : (g + 1) * P].bitcast(FP8X4),
                         lhsT_scale=toks[(b, pt)][:, g * P : (g + 1) * P],
-                        rhs=wcodes[(stream, j)][:, g, :].bitcast(FP8X4),
-                        rhs_scale=wscales[(stream, j)][:, g, :],
+                        rhs=wcodes[(stream, j, g)][:].bitcast(FP8X4),
+                        rhs_scale=wscales[(stream, j, g)][:],
                         start=(g == 0),
                         stop=(g == 1),
                     )
-                banks.append(acc)
-            accs[i] = banks
-
-        def sq(i):
+                accs.append(acc)
             ss = small.tile([P, 8], F32, name="ss")
             for k in range(2):
                 for h in range(4):
-                    junk = small.tile([P, HD], BF16, name="junk")
+                    junk = stage.tile([P, HD], BF16, name="junk")
                     nc.scalar.activation(
                         out=junk[:],
-                        in_=accs[i][k][:, h * HD : (h + 1) * HD],
+                        in_=accs[k][:, h * HD : (h + 1) * HD],
                         func=ACT.Square,
                         accum_out=ss[:, 4 * k + h : 4 * k + h + 1],
                     )
             rstd = small.tile([P, 8], F32, name="rstd")
             nc.scalar.activation(out=rstd[:], in_=ss[:], func=ACT.Abs_reciprocal_sqrt, scale=1.0 / HD, bias=EPS)
-            rstds[i] = rstd
-
-        uvs = {}
-
-        def rot(rotp, i, first, last):
-            stream, j, tiles = pairs[i]
-            qk = j // 2
-            if first == 0:
-                uvs[i] = rotp.tile([P, 8, 2, HD], F32, name="uv")
-            for hh in range(first, last):
-                k = hh // 4
-                h = hh % 4
-                b, pt = tiles[k]
-                nc.vector.scalar_tensor_tensor(
-                    out=uvs[i][:, hh],
-                    in0=accs[i][k][:, h * HD : (h + 1) * HD].rearrange("p (o d) -> p o d", o=1).to_broadcast([P, 2, HD]),
-                    scalar=rstds[i][:, hh : hh + 1],
-                    in1=tabA[(b, pt, qk)][:].rearrange("p r j e -> p r (j e)"),
-                    op0=ALU.mult,
-                    op1=ALU.mult,
-                )
-
-        def add_store(rotp, i, eng, split):
-            stream, j, tiles = pairs[i]
-            qk = j // 2
-            h0 = 4 * (j % 2)
-            r = rotp.tile([P, 8, 64, 2], F32, name="r")
-            uv5 = uvs[i][:].rearrange("p h r (j e) -> p h r j e", e=2)
-            if not split:
-                eng.tensor_tensor(out=r[:], in0=uv5[:, :, 0], in1=uv5[:, :, 1, :, ::-1], op=ALU.add)
+            uv = stage.tile([P, 8, 2, HD], F32, name="uv")
             for k in range(2):
                 b, pt = tiles[k]
-                hs = slice(4 * k, 4 * k + 4)
-                if split:
-                    eng.tensor_tensor(out=r[:, hs], in0=uv5[:, hs, 0], in1=uv5[:, hs, 1, :, ::-1], op=ALU.add)
+                for h in range(4):
+                    nc.vector.scalar_tensor_tensor(
+                        out=uv[:, 4 * k + h],
+                        in0=accs[k][:, h * HD : (h + 1) * HD].rearrange("p (o d) -> p o d", o=1).to_broadcast([P, 2, HD]),
+                        scalar=rstd[:, 4 * k + h : 4 * k + h + 1],
+                        in1=tabA[(b, pt, qk)][:].rearrange("p r j e -> p r (j e)"),
+                        op0=ALU.mult,
+                        op1=ALU.mult,
+                    )
+            uv5 = uv[:].rearrange("p h r (j e) -> p h r j e", e=2)
+            r = stage.tile([P, 8, 64, 2], F32, name="r")
+            if not own:
+                nc.gpsimd.tensor_tensor(out=r[:], in0=uv5[:, :, 0], in1=uv5[:, :, 1, :, ::-1], op=ALU.add)
+            for k in range(2):
+                b, pt = tiles[k]
+                if own:
+                    hs = slice(4 * k, 4 * k + 4)
+                    nc.vector.tensor_tensor(out=r[:, hs], in0=uv5[:, hs, 0], in1=uv5[:, hs, 1, :, ::-1], op=ALU.add)
                 nc.sync.dma_start(
                     out=outs[qk][b, h0 : h0 + 4, pt * P : (pt + 1) * P, :].rearrange("h p d -> p h d"),
-                    in_=r[:, hs].rearrange("p h j e -> p h (j e)"),
+                    in_=r[:, 4 * k : 4 * k + 4].rearrange("p h j e -> p h (j e)"),
                 )
 
-        XT = [(b, pt) for b in range(2) for pt in range(1, 4)]
-
-        with tc.tile_pool(name="early", bufs=1) as early:
-            wx_scale = keep.tile([P, 2, 4], F32, name="wx_scale")
-            nc.sync.dma_start(out=wx_scale[:], in_=Wqk_x_scale.rearrange("(g p t) o -> p g (t o)", p=P, t=4))
-            load_wc(early, 0)
-            load_wx(0)
-            load_wc(early, 1)
-            load_tok(early, 0, 0)
-            load_tok(early, 1, 0)
-            load_wc(early, 2)
-            load_wx(1)
-            load_wc(early, 3)
-            for i, vec in enumerate((qn_c, kn_c, qn_x, kn_x)):
-                nc.sync.dma_start(out=grow[0:1, i * HD : (i + 1) * HD], in_=vec.rearrange("(o d) -> o d", o=1))
-            fr = keep.tile([P, 8, 64, 2, 1], BF16, name="fr")
-            nc.sync.dma_start(
-                out=fr[:].rearrange("p t j c o -> p t (j c o)"),
-                in_=freqs_cis.rearrange("b (t p) j c -> p (b t) (j c)", p=P),
-            )
-            for b, pt in XT:
-                load_tok(early, b, pt)
-            load_wx(2)
-            load_wx(3)
-
-            def wgc(j):
-                wgrp[("c", j)] = early.tile([P, 2, CH, 4], BF16, name="wgc", bufs=2, align_bytes=64)
-
-            wgc(0)
-            wc_interleave(0, 0)
-            wc_interleave(0, 1)
-            wx_group(0)
-            wx_widen(0, 0, 0, 4)
-            wx_widen(0, 1, 0, 4)
-            wx_strided(0, 0)
-            wx_strided(0, 1)
-            wgc(1)
-            wc_interleave(1, 0)
-            w_quant("c", 0)
-            wc_interleave(1, 1)
-            tok_turn(0, 0)
-            tok_turn(1, 0)
-            tok_copy(early, 0, 0)
-            tok_copy(early, 1, 0)
-            for j in range(2, NCH):
-                wgc(j)
-                wc_interleave(j, 0)
-                w_quant("c", j - 1)
-                wc_interleave(j, 1)
-            gains_spread()
-            wx_group(1)
-            wx_widen(1, 0, 0, 4)
-            wx_permute(1, 0)
-            wx_widen(1, 1, 0, 4)
-            wx_permute(1, 1)
-            wx_empty(1, 0)
-            wx_empty(1, 1)
-            tok_quant(0, 0)
-            tok_quant(1, 0)
-            w_quant("c", NCH - 1)
-            gains_copy()
-            build_tables(0, 0)
-            build_tables(1, 0)
-            for b, pt in XT:
-                tok_turn(b, pt)
-                tok_copy(early, b, pt)
-            w_quant("x", 0)
-            for b, pt in XT:
+        prep_wc(0)
+        prep_tok(0, 0)
+        prep_tok(1, 0)
+        prep_wx(0)
+        prep_wc(1)
+        prep_wc(2)
+        prep_wc(3)
+        prep_gains()
+        build_tables(0, 0)
+        build_tables(1, 0)
+        for j in range(NCH):
+            pair("c", ((0, 0), (1, 0)), j)
+        for b in range(2):
+            for pt in range(1, 4):
+                prep_tok(b, pt)
                 build_tables(b, pt)
-            w_quant("x", 1)
-            for b, pt in XT:
-                tok_quant(b, pt)
-
-        def late_step(k):
-            j = 2 + k // 6
-            s = k % 6
-            if s == 0:
-                wx_widen(j, 0, 0, 2)
-            elif s == 1:
-                wx_widen(j, 0, 2, 4)
-                wx_permute(j, 0)
-            elif s == 2:
-                wx_widen(j, 1, 0, 2)
-            elif s == 3:
-                wx_group(j)
-                wx_empty(j, 0)
-            elif s == 4:
-                wx_widen(j, 1, 2, 4)
-                wx_permute(j, 1)
-            else:
-                wx_empty(j, 1)
-
-        ON_POOL = (0, 1, 3, 4, 6, 7, 9, 10, 12, 13)
-        STEPS = (2, 1, 1, 2, 1, 1, 2, 1, 1, 0, 0, 0, 0, 0, 0, 0, 0)
-        with tc.tile_pool(name="rotp", bufs=4) as rotp:
-            mm(0)
-            mm(1)
-            sq(0)
-            done = 0
-            for k in range(STEPS[0]):
-                late_step(done)
-                done += 1
-            waiting = []
-            quant_at = {6: 2, 9: 3}
-            for i in range(NP):
-                if i + 2 < NP:
-                    mm(i + 2)
-                if i + 1 < NP:
-                    sq(i + 1)
-                for k in range(STEPS[i + 1]):
-                    late_step(done)
-                    done += 1
-                if i in ON_POOL:
-                    rot(rotp, i, 0, 7)
-                    for w in waiting:
-                        add_store(rotp, w, nc.vector, False)
-                    waiting = []
-                    if i in quant_at:
-                        w_quant("x", quant_at[i])
-                    rot(rotp, i, 7, 8)
-                    add_store(rotp, i, nc.gpsimd, False)
-                else:
-                    rot(rotp, i, 0, 8)
-                    waiting.append(i)
-            for w in waiting[:-1]:
-                add_store(rotp, w, nc.vector, False)
-            add_store(rotp, waiting[-1], nc.vector, True)
+        prep_wx(1)
+        for j in range(NCH):
+            if j + 2 < NCH:
+                prep_wx(j + 2)
+            for n, tiles in enumerate((((0, 1), (0, 2)), ((0, 3), (1, 1)), ((1, 2), (1, 3)))):
+                pair("x", tiles, j, own=(j == NCH - 1 and n >= 1))

@@ -117,8 +117,8 @@ def tile_dualstreamattentionwithrotaryembedding_pa_kernel(
 
         def interleave_quantize(stream, j, g, src, eng):
             grouped = stage.tile([P, 4 * CH], BF16, name="wg", align_bytes=64)
-            o = grouped[:].rearrange("p (n t) -> p n t", t=4)
-            i = src[:].rearrange("p t n -> p n t")
+            o = grouped[:].rearrange("p (c i t) -> p c t i", i=4, t=4)
+            i = src[:].rearrange("p t (c i) -> p c t i", i=4)
             if eng == "V":
                 nc.vector.tensor_copy(out=o, in_=i)
             else:

@@ -21,7 +21,7 @@ CH = 512
 NCH = 4
 EPS = 1e-6
 
-X_INTERLEAVE = {(3, 0): "V", (3, 1): "V"}
+X_INTERLEAVE = {(2, 0): "V", (2, 1): "V", (3, 0): "V", (3, 1): "V"}
 
 
 def tile_dualstreamattentionwithrotaryembedding_pa_kernel(

@@ -68,21 +68,22 @@ def tile_dualstreamattentionwithrotaryembedding_pa_kernel(
                 nc.sync.dma_start(out=t[:], in_=x[b, (pt - 1) * P : pt * P, :])
             tok[(b, pt)] = t
 
-        load_wc(0)
-        wx_scale = keep.tile([P, 2, 4], F32, name="wx_scale")
-        nc.sync.dma_start(out=wx_scale[:], in_=Wqk_x_scale.rearrange("(g p t) o -> p g (t o)", p=P, t=4))
-        load_wx(0)
-        load_tok(0, 0)
-        load_tok(1, 0)
-        load_wc(1)
         gw = keep.tile([P, 4, 64, 2], BF16, name="gw")
         for i, vec in enumerate((qn_c, kn_c, qn_x, kn_x)):
             nc.sync.dma_start(out=gw[:, i].rearrange("p j e -> p (j e)"), in_=vec.partition_broadcast(P))
         fr = keep.tile([P, 8, 64, 2, 1], BF16, name="fr")
-        nc.sync.dma_start(
-            out=fr[:].rearrange("p t j c o -> p t (j c o)"),
-            in_=freqs_cis.rearrange("b (t p) j c -> p (b t) (j c)", p=P),
-        )
+        fr_rows = fr[:].rearrange("p (b t) j c o -> p b t (j c o)", b=2)
+        fr_view = freqs_cis.rearrange("b (t p) j c -> p b t (j c)", p=P)
+        nc.sync.dma_start(out=fr_rows[:, :, 0], in_=fr_view[:, :, 0])
+        for b in range(2):
+            nc.sync.dma_start(out=fr_rows[:, b, 1:4], in_=fr_view[:, b, 1:4])
+        wx_scale = keep.tile([P, 2, 4], F32, name="wx_scale")
+        nc.sync.dma_start(out=wx_scale[:], in_=Wqk_x_scale.rearrange("(g p t) o -> p g (t o)", p=P, t=4))
+        load_wx(0)
+        load_wc(0)
+        load_tok(0, 0)
+        load_tok(1, 0)
+        load_wc(1)
         load_wx(1)
         load_wc(2)
         load_wc(3)
@@ -218,6 +219,10 @@ def tile_dualstreamattentionwithrotaryembedding_pa_kernel(
                     in_=r[:, 4 * k : 4 * k + 4].rearrange("p h j e -> p h (j e)"),
                 )
 
+        prep_gains()
+        for pt in range(4):
+            for b in range(2):
+                build_tables(b, pt)
         prep_wc(0)
         prep_tok(0, 0)
         prep_tok(1, 0)
@@ -225,15 +230,11 @@ def tile_dualstreamattentionwithrotaryembedding_pa_kernel(
         prep_wc(1)
         prep_wc(2)
         prep_wc(3)
-        prep_gains()
-        build_tables(0, 0)
-        build_tables(1, 0)
         for j in range(NCH):
             pair("c", ((0, 0), (1, 0)), j)
         for b in range(2):
             for pt in range(1, 4):
                 prep_tok(b, pt)
-                build_tables(b, pt)
         prep_wx(1)
         for j in range(NCH):
             if j + 2 < NCH:

@@ -68,9 +68,12 @@ def tile_dualstreamattentionwithrotaryembedding_pa_kernel(
                 nc.sync.dma_start(out=t[:], in_=x[b, (pt - 1) * P : pt * P, :])
             tok[(b, pt)] = t
 
-        gw = keep.tile([P, 4, 64, 2], BF16, name="gw")
+        grow = keep.tile([P, 4, HD], BF16, name="grow")
+        nc.vector.memset(grow[:], 0.0)
+        ones_b = keep.tile([P, P], BF16, name="ones_b")
+        nc.vector.memset(ones_b[:], 1.0)
         for i, vec in enumerate((qn_c, kn_c, qn_x, kn_x)):
-            nc.sync.dma_start(out=gw[:, i].rearrange("p j e -> p (j e)"), in_=vec.partition_broadcast(P))
+            nc.sync.dma_start(out=grow[0:1, i, :], in_=vec.rearrange("(o d) -> o d", o=1))
         fr = keep.tile([P, 8, 64, 2, 1], BF16, name="fr")
         fr_rows = fr[:].rearrange("p (b t) j c o -> p b t (j c o)", b=2)
         fr_view = freqs_cis.rearrange("b (t p) j c -> p b t (j c)", p=P)
@@ -149,10 +152,18 @@ def tile_dualstreamattentionwithrotaryembedding_pa_kernel(
         g2 = keep.tile([P, 4, 2, 64, 2], F32, name="g2")
 
         def prep_gains():
-            nc.vector.tensor_copy(out=g2[:, :, 0], in_=gw[:])
-            nc.vector.tensor_copy(out=g2[:, :, 1, :, 0], in_=gw[:, :, :, 0])
+            spread = psum.tile([P, 4, 64, 2], F32, name="spread", tag="bank")
+            nc.tensor.matmul(
+                out=spread[:].rearrange("p i j e -> p (i j e)"),
+                lhsT=ones_b[:],
+                rhs=grow[:].rearrange("p i d -> p (i d)"),
+                start=True,
+                stop=True,
+            )
+            nc.vector.tensor_copy(out=g2[:, :, 0], in_=spread[:])
+            nc.vector.tensor_copy(out=g2[:, :, 1, :, 0], in_=spread[:, :, :, 0])
             nc.vector.tensor_scalar(
-                out=g2[:, :, 1, :, 1], in0=gw[:, :, :, 1], scalar1=-1.0, scalar2=None, op0=ALU.mult
+                out=g2[:, :, 1, :, 1], in0=spread[:, :, :, 1], scalar1=-1.0, scalar2=None, op0=ALU.mult
             )
 
         def build_tables(b, pt):

@@ -8,6 +8,7 @@ FLOPS = 2 * 1024 * 1024 * 2048
 F32 = mybir.dt.float32
 BF16 = mybir.dt.bfloat16
 U32 = mybir.dt.uint32
+I32 = mybir.dt.int32
 U8 = mybir.dt.uint8
 FP8 = mybir.dt.float8_e4m3fn
 FP8X4 = mybir.dt.float8_e4m3fn_x4
@@ -35,6 +36,10 @@ def tile_dualstreamattentionwithrotaryembedding_pa_kernel(
         small = ctx.enter_context(tc.tile_pool(name="small", bufs=8))
         psum = ctx.enter_context(tc.psum_pool(name="psum", bufs=8))
 
+        grow = keep.tile([P, 4, HD], BF16, name="grow")
+        nc.vector.memset(grow[:].rearrange("p i d -> p (i d)").bitcast(I32), 0)
+        ones_b = keep.tile([P, P], BF16, name="ones_b")
+        nc.gpsimd.memset(ones_b[:], 1.0)
         ident = keep.tile([P, P], F32, name="ident")
         make_identity(nc, ident[:])
         one = keep.tile([P, 1], F32, name="one")
@@ -68,10 +73,8 @@ def tile_dualstreamattentionwithrotaryembedding_pa_kernel(
                 nc.sync.dma_start(out=t[:], in_=x[b, (pt - 1) * P : pt * P, :])
             tok[(b, pt)] = t
 
-        grow = keep.tile([P, 4, HD], BF16, name="grow")
-        nc.vector.memset(grow[:], 0.0)
-        ones_b = keep.tile([P, P], BF16, name="ones_b")
-        nc.vector.memset(ones_b[:], 1.0)
+        wx_scale = keep.tile([P, 2, 8], F32, name="wx_scale")
+        nc.sync.dma_start(out=wx_scale[:, :, 0:4], in_=Wqk_x_scale.rearrange("(g p t) o -> p g (t o)", p=P, t=4))
         for i, vec in enumerate((qn_c, kn_c, qn_x, kn_x)):
             nc.sync.dma_start(out=grow[0:1, i, :], in_=vec.rearrange("(o d) -> o d", o=1))
         fr = keep.tile([P, 8, 64, 2, 1], BF16, name="fr")
@@ -80,8 +83,6 @@ def tile_dualstreamattentionwithrotaryembedding_pa_kernel(
         nc.sync.dma_start(out=fr_rows[:, :, 0], in_=fr_view[:, :, 0])
         for b in range(2):
             nc.sync.dma_start(out=fr_rows[:, b, 1:4], in_=fr_view[:, b, 1:4])
-        wx_scale = keep.tile([P, 2, 4], F32, name="wx_scale")
-        nc.sync.dma_start(out=wx_scale[:], in_=Wqk_x_scale.rearrange("(g p t) o -> p g (t o)", p=P, t=4))
         load_wx(0)
         load_wc(0)
         load_tok(0, 0)
@@ -149,10 +150,10 @@ def tile_dualstreamattentionwithrotaryembedding_pa_kernel(
                     )
                 interleave_quantize("x", j, g, wide, X_INTERLEAVE.get((j, g), "S"))
 
-        g2 = keep.tile([P, 4, 2, 64, 2], F32, name="g2")
+        g2 = keep.tile([P, 4, 2, 64, 2], BF16, name="g2")
 
         def prep_gains():
-            spread = psum.tile([P, 4, 64, 2], F32, name="spread", tag="bank")
+            spread = psum.tile([P, 4, 64, 2], BF16, name="spread", tag="bank")
             nc.tensor.matmul(
                 out=spread[:].rearrange("p i j e -> p (i j e)"),
                 lhsT=ones_b[:],

@@ -22,7 +22,7 @@ CH = 512
 NCH = 4
 EPS = 1e-6
 
-X_INTERLEAVE = {(2, 0): "V", (2, 1): "V", (3, 0): "V", (3, 1): "V"}
+X_CHUNKS_ON_VECTOR = 2
 
 
 def tile_dualstreamattentionwithrotaryembedding_pa_kernel(
@@ -54,10 +54,10 @@ def tile_dualstreamattentionwithrotaryembedding_pa_kernel(
         tok = {}
 
         def load_wc(j):
+            t = stage.tile([P, 2, 4, CH], BF16, name="wc_raw", tag="big")
             for g in range(2):
-                t = keep.tile([P, 4, CH], BF16, name="wc_raw_%d_%d" % (j, g))
-                nc.sync.dma_start(out=t[:], in_=wc_view[g][:, :, j * CH : (j + 1) * CH])
-                wc_raw[(j, g)] = t
+                nc.sync.dma_start(out=t[:, g], in_=wc_view[g][:, :, j * CH : (j + 1) * CH])
+                wc_raw[(j, g)] = t[:, g]
 
         def load_wx(j):
             for g in range(2):
@@ -90,10 +90,10 @@ def tile_dualstreamattentionwithrotaryembedding_pa_kernel(
         load_wc(1)
         load_wx(1)
         load_wc(2)
-        load_wc(3)
         for b in range(2):
             for pt in range(1, 4):
                 load_tok(b, pt)
+        load_wc(3)
         load_wx(2)
         load_wx(3)
 
@@ -103,52 +103,74 @@ def tile_dualstreamattentionwithrotaryembedding_pa_kernel(
         wscales = {}
         tabA = {}
 
-        def prep_tok(b, pt):
+        tok_grouped = {}
+
+        def turn_tok(b, pt):
             words = tok[(b, pt)][:].bitcast(F32)
             xt = psum.tile([P, 4, P], F32, name="xt", tag="bank")
             for g in range(2):
                 for u in range(2):
                     nc.tensor.transpose(xt[:, 2 * g + u, :], words[:, 256 * g + u : 256 * (g + 1) : 2], ident[:])
-            grouped = stage.tile([P, D], BF16, name="tokg", align_bytes=64)
+            grouped = stage.tile([P, D], BF16, name="tokg", bufs=6, align_bytes=64)
             nc.scalar.copy(
                 out=grouped[:].bitcast(F32).rearrange("p (g r u) -> p g r u", g=2, u=2),
                 in_=xt[:].rearrange("p (g u) r -> p g r u", g=2),
             )
+            tok_grouped[(b, pt)] = grouped
+
+        def quantize_tok(b, pt):
             codes = keep.tile([P, 2 * P], U32, name="tokc_%d_%d" % (b, pt), align_bytes=64)
             scl = keep.tile([P, 2 * P], U8, name="toks_%d_%d" % (b, pt), align_bytes=64)
-            nc.vector.quantize_mx(out=codes[:].bitcast(FP8X4), scales=scl[:], in_=grouped[:])
+            nc.vector.quantize_mx(out=codes[:].bitcast(FP8X4), scales=scl[:], in_=tok_grouped[(b, pt)][:])
             tokc[(b, pt)] = codes
             toks[(b, pt)] = scl
 
-        def interleave_quantize(stream, j, g, src, eng):
-            grouped = stage.tile([P, 4 * CH], BF16, name="wg", align_bytes=64)
+        grouped_w = {}
+
+        def interleave(stream, j, g, src, eng):
+            grouped = stage.tile([P, 4 * CH], BF16, name="wg_" + eng, align_bytes=64)
             o = grouped[:].rearrange("p (c i t) -> p c t i", i=4, t=4)
-            i = src[:].rearrange("p t (c i) -> p c t i", i=4)
+            i = src.rearrange("p t (c i) -> p c t i", i=4)
             if eng == "V":
                 nc.vector.tensor_copy(out=o, in_=i)
             else:
                 nc.scalar.copy(out=o, in_=i)
+            grouped_w[(stream, j, g)] = grouped
+
+        def quantize_w(stream, j, g):
+            grouped = grouped_w[(stream, j, g)]
             codes = keep.tile([P, CH], U32, name="wcod_%s_%d_%d" % (stream, j, g), align_bytes=64)
             scl = keep.tile([P, CH], U8, name="wscl_%s_%d_%d" % (stream, j, g), align_bytes=64)
             nc.vector.quantize_mx(out=codes[:].bitcast(FP8X4), scales=scl[:], in_=grouped[:])
             wcodes[(stream, j, g)] = codes
             wscales[(stream, j, g)] = scl
 
-        def prep_wc(j):
-            for g in range(2):
-                interleave_quantize("c", j, g, wc_raw[(j, g)], "V")
+        wide = {}
 
-        def prep_wx(j):
+        def widen(j):
             for g in range(2):
-                wide = stage.tile([P, 4, CH], BF16, name="wide")
+                w = stage.tile([P, 4, CH], BF16, name="wide", bufs=6)
                 for t in range(4):
                     nc.scalar.activation(
-                        out=wide[:, t, :],
+                        out=w[:, t, :],
                         in_=wx_bytes[(j, g)][:, t, :].bitcast(FP8),
                         func=ACT.Copy,
                         scale=wx_scale[:, g, t : t + 1],
                     )
-                interleave_quantize("x", j, g, wide, X_INTERLEAVE.get((j, g), "S"))
+                wide[(j, g)] = w[:]
+
+        def prep_wc(j):
+            interleave("c", j, 0, wc_raw[(j, 0)], "V")
+            interleave("c", j, 1, wc_raw[(j, 1)], "V")
+            quantize_w("c", j, 0)
+            quantize_w("c", j, 1)
+
+        def prep_wx(j):
+            eng = "V" if j < X_CHUNKS_ON_VECTOR else "S"
+            interleave("x", j, 0, wide[(j, 0)], eng)
+            interleave("x", j, 1, wide[(j, 1)], eng)
+            quantize_w("x", j, 0)
+            quantize_w("x", j, 1)
 
         g2 = keep.tile([P, 4, 2, 64, 2], BF16, name="g2")
 
@@ -176,9 +198,7 @@ def tile_dualstreamattentionwithrotaryembedding_pa_kernel(
                 nc.vector.tensor_tensor(out=ta[:], in0=g2[:, 2 * s + qk], in1=cs, op=ALU.mult)
                 tabA[(b, pt, qk)] = ta
 
-        def pair(stream, tiles, j, own=False):
-            qk = j // 2
-            h0 = 4 * (j % 2)
+        def project(stream, tiles, j):
             accs = []
             for b, pt in tiles:
                 acc = psum.tile([P, CH], F32, name="acc", tag="bank")
@@ -205,7 +225,12 @@ def tile_dualstreamattentionwithrotaryembedding_pa_kernel(
                     )
             rstd = small.tile([P, 8], F32, name="rstd")
             nc.scalar.activation(out=rstd[:], in_=ss[:], func=ACT.Abs_reciprocal_sqrt, scale=1.0 / HD, bias=EPS)
-            uv = stage.tile([P, 8, 2, HD], F32, name="uv")
+            return accs, rstd
+
+        def rotate(accs, rstd, tiles, j, own=False):
+            qk = j // 2
+            h0 = 4 * (j % 2)
+            uv = stage.tile([P, 8, 2, HD], F32, name="uv", tag="big")
             for k in range(2):
                 b, pt = tiles[k]
                 for h in range(4):
@@ -218,7 +243,7 @@ def tile_dualstreamattentionwithrotaryembedding_pa_kernel(
                         op1=ALU.mult,
                     )
             uv5 = uv[:].rearrange("p h r (j e) -> p h r j e", e=2)
-            r = stage.tile([P, 8, 64, 2], F32, name="r")
+            r = stage.tile([P, 8, 64, 2], F32, name="r", bufs=3)
             if not own:
                 nc.gpsimd.tensor_tensor(out=r[:], in0=uv5[:, :, 0], in1=uv5[:, :, 1, :, ::-1], op=ALU.add)
             for k in range(2):
@@ -231,25 +256,38 @@ def tile_dualstreamattentionwithrotaryembedding_pa_kernel(
                     in_=r[:, 4 * k : 4 * k + 4].rearrange("p h j e -> p h (j e)"),
                 )
 
+        C_TILES = ((0, 0), (1, 0))
+        X_TILES = (((0, 1), (0, 2)), ((0, 3), (1, 1)), ((1, 2), (1, 3)))
+
         prep_gains()
         for pt in range(4):
             for b in range(2):
                 build_tables(b, pt)
+        for b in range(2):
+            turn_tok(b, 0)
+        widen(0)
         prep_wc(0)
-        prep_tok(0, 0)
-        prep_tok(1, 0)
-        prep_wx(0)
-        prep_wc(1)
-        prep_wc(2)
-        prep_wc(3)
-        for j in range(NCH):
-            pair("c", ((0, 0), (1, 0)), j)
+        for b in range(2):
+            quantize_tok(b, 0)
+        for j in range(1, NCH):
+            prep_wc(j)
         for b in range(2):
             for pt in range(1, 4):
-                prep_tok(b, pt)
-        prep_wx(1)
+                turn_tok(b, pt)
+        widen(1)
+        c_banks = [project("c", C_TILES, j) for j in range(NCH)]
+        for b in range(2):
+            for pt in range(1, 4):
+                quantize_tok(b, pt)
+        for j in range(X_CHUNKS_ON_VECTOR):
+            prep_wx(j)
+        widen(2)
+        prep_wx(2)
         for j in range(NCH):
-            if j + 2 < NCH:
-                prep_wx(j + 2)
-            for n, tiles in enumerate((((0, 1), (0, 2)), ((0, 3), (1, 1)), ((1, 2), (1, 3)))):
-                pair("x", tiles, j, own=(j == NCH - 1 and n >= 1))
+            rotate(*c_banks[j], C_TILES, j)
+        for j in range(NCH):
+            if j == 1:
+                widen(3)
+                prep_wx(3)
+            for n, tiles in enumerate(X_TILES):
+                rotate(*project("x", tiles, j), tiles, j, own=(j == NCH - 1 and n >= 1))

@@ -22,7 +22,10 @@ CH = 512
 NCH = 4
 EPS = 1e-6
 
-X_CHUNKS_ON_VECTOR = 2
+INTERLEAVER = {
+    "c": ("V", "V", "V", "T"),
+    "x": ("V", "T", "T", "S"),
+}
 
 
 def tile_dualstreamattentionwithrotaryembedding_pa_kernel(
@@ -42,6 +45,8 @@ def tile_dualstreamattentionwithrotaryembedding_pa_kernel(
         nc.gpsimd.memset(ones_b[:], 1.0)
         ident = keep.tile([P, P], F32, name="ident")
         make_identity(nc, ident[:])
+        ident_b = keep.tile([P, P], BF16, name="ident_b")
+        make_identity(nc, ident_b[:])
         one = keep.tile([P, 1], F32, name="one")
         nc.vector.memset(one[:], 1.0)
         warm = keep.tile([P, 1], F32, name="warm")
@@ -74,20 +79,23 @@ def tile_dualstreamattentionwithrotaryembedding_pa_kernel(
             tok[(b, pt)] = t
 
         wx_scale = keep.tile([P, 2, 8], F32, name="wx_scale")
-        nc.sync.dma_start(out=wx_scale[:, :, 0:4], in_=Wqk_x_scale.rearrange("(g p t) o -> p g (t o)", p=P, t=4))
-        for i, vec in enumerate((qn_c, kn_c, qn_x, kn_x)):
-            nc.sync.dma_start(out=grow[0:1, i, :], in_=vec.rearrange("(o d) -> o d", o=1))
         fr = keep.tile([P, 8, 64, 2, 1], BF16, name="fr")
-        fr_rows = fr[:].rearrange("p (b t) j c o -> p b t (j c o)", b=2)
-        fr_view = freqs_cis.rearrange("b (t p) j c -> p b t (j c)", p=P)
-        nc.sync.dma_start(out=fr_rows[:, :, 0], in_=fr_view[:, :, 0])
-        for b in range(2):
-            nc.sync.dma_start(out=fr_rows[:, b, 1:4], in_=fr_view[:, b, 1:4])
-        load_wx(0)
+
+        def load_table_inputs():
+            for i, vec in enumerate((qn_c, kn_c, qn_x, kn_x)):
+                nc.sync.dma_start(out=grow[0:1, i, :], in_=vec.rearrange("(o d) -> o d", o=1))
+            nc.sync.dma_start(
+                out=fr[:].rearrange("p f j c o -> p f (j c o)"),
+                in_=freqs_cis.rearrange("b (t p) j c -> p (b t) (j c)", p=P),
+            )
+
         load_wc(0)
+        nc.sync.dma_start(out=wx_scale[:, :, 0:4], in_=Wqk_x_scale.rearrange("(g p t) o -> p g (t o)", p=P, t=4))
+        load_wx(0)
         load_tok(0, 0)
         load_tok(1, 0)
         load_wc(1)
+        load_table_inputs()
         load_wx(1)
         load_wc(2)
         for b in range(2):
@@ -133,8 +141,23 @@ def tile_dualstreamattentionwithrotaryembedding_pa_kernel(
             i = src.rearrange("p t (c i) -> p c t i", i=4)
             if eng == "V":
                 nc.vector.tensor_copy(out=o, in_=i)
-            else:
+            elif eng == "S":
                 nc.scalar.copy(out=o, in_=i)
+            else:
+                for h in range(2):
+                    bank = psum.tile([P, 2, 4 * P], BF16, name="turned", tag="bank")
+                    for q in range(2):
+                        cols = slice((2 * h + q) * P, (2 * h + q + 1) * P)
+                        nc.tensor.matmul(
+                            out=bank[:, q],
+                            lhsT=ident_b[:],
+                            rhs=src[:, :, cols].rearrange("p t n -> p n t"),
+                            start=True,
+                            stop=True,
+                        )
+                    nc.scalar.copy(
+                        out=grouped[:, h * 2 * CH : (h + 1) * 2 * CH], in_=bank[:].rearrange("p q m -> p (q m)")
+                    )
             grouped_w[(stream, j, g)] = grouped
 
         def quantize_w(stream, j, g):
@@ -159,16 +182,19 @@ def tile_dualstreamattentionwithrotaryembedding_pa_kernel(
                     )
                 wide[(j, g)] = w[:]
 
-        def prep_wc(j):
-            interleave("c", j, 0, wc_raw[(j, 0)], "V")
-            interleave("c", j, 1, wc_raw[(j, 1)], "V")
+        def interleave_wc(j):
+            for g in range(2):
+                interleave("c", j, g, wc_raw[(j, g)], INTERLEAVER["c"][j])
+
+        def quantize_wc(j):
             quantize_w("c", j, 0)
             quantize_w("c", j, 1)
 
-        def prep_wx(j):
-            eng = "V" if j < X_CHUNKS_ON_VECTOR else "S"
-            interleave("x", j, 0, wide[(j, 0)], eng)
-            interleave("x", j, 1, wide[(j, 1)], eng)
+        def interleave_wx(j):
+            for g in range(2):
+                interleave("x", j, g, wide[(j, g)], INTERLEAVER["x"][j])
+
+        def quantize_wx(j):
             quantize_w("x", j, 0)
             quantize_w("x", j, 1)
 
@@ -259,35 +285,48 @@ def tile_dualstreamattentionwithrotaryembedding_pa_kernel(
         C_TILES = ((0, 0), (1, 0))
         X_TILES = (((0, 1), (0, 2)), ((0, 3), (1, 1)), ((1, 2), (1, 3)))
 
+        for b in range(2):
+            turn_tok(b, 0)
+        widen(0)
+        interleave_wc(0)
+        quantize_wc(0)
+        for b in range(2):
+            quantize_tok(b, 0)
+        interleave_wc(1)
+        quantize_wc(1)
         prep_gains()
         for pt in range(4):
             for b in range(2):
                 build_tables(b, pt)
-        for b in range(2):
-            turn_tok(b, 0)
-        widen(0)
-        prep_wc(0)
-        for b in range(2):
-            quantize_tok(b, 0)
-        for j in range(1, NCH):
-            prep_wc(j)
+        interleave_wc(2)
+        quantize_wc(2)
         for b in range(2):
             for pt in range(1, 4):
                 turn_tok(b, pt)
         widen(1)
-        c_banks = [project("c", C_TILES, j) for j in range(NCH)]
+        interleave_wx(1)
+        interleave_wc(3)
+        widen(2)
+        interleave_wx(2)
+        interleave_wx(0)
+        quantize_wx(0)
         for b in range(2):
             for pt in range(1, 4):
                 quantize_tok(b, pt)
-        for j in range(X_CHUNKS_ON_VECTOR):
-            prep_wx(j)
-        widen(2)
-        prep_wx(2)
-        for j in range(NCH):
-            rotate(*c_banks[j], C_TILES, j)
-        for j in range(NCH):
-            if j == 1:
+        quantize_wx(1)
+        quantize_wc(3)
+        quantize_wx(2)
+        c_banks = [project("c", C_TILES, j) for j in range(NCH)]
+        pairs = [(C_TILES, j, c_banks[j]) for j in range(NCH)]
+        x_pairs = [(tiles, j) for j in range(NCH) for tiles in X_TILES]
+        for i in range(len(pairs) + len(x_pairs)):
+            tiles, j, banks = pairs[i]
+            rotate(*banks, tiles, j, own=(i >= 14))
+            if i < len(x_pairs):
+                tiles, j = x_pairs[i]
+                pairs.append((tiles, j, project("x", tiles, j)))
+            if i == 1:
                 widen(3)
-                prep_wx(3)
-            for n, tiles in enumerate(X_TILES):
-                rotate(*project("x", tiles, j), tiles, j, own=(j == NCH - 1 and n >= 1))
+            if i == 3:
+                interleave_wx(3)
+                quantize_wx(3)

@@ -149,9 +149,9 @@ def tile_dualstreamattentionwithrotaryembedding_pa_kernel(
                     for q in range(2):
                         cols = slice((2 * h + q) * P, (2 * h + q + 1) * P)
                         nc.tensor.matmul(
-                            out=bank[:, q],
+                            out=bank[:, q].rearrange("p (n t) -> p t n", t=4),
                             lhsT=ident_b[:],
-                            rhs=src[:, :, cols].rearrange("p t n -> p n t"),
+                            rhs=src[:, :, cols],
                             start=True,
                             stop=True,
                         )

@@ -23,8 +23,8 @@ NCH = 4
 EPS = 1e-6
 
 INTERLEAVER = {
-    "c": ("V", "V", "V", "T"),
-    "x": ("V", "T", "T", "S"),
+    "c": ("V", "T", "T", "T"),
+    "x": ("V", "V", "V", "S"),
 }
 
 
@@ -96,12 +96,12 @@ def tile_dualstreamattentionwithrotaryembedding_pa_kernel(
         load_tok(1, 0)
         load_wc(1)
         load_table_inputs()
-        load_wx(1)
         load_wc(2)
+        load_wx(1)
+        load_wc(3)
         for b in range(2):
             for pt in range(1, 4):
                 load_tok(b, pt)
-        load_wc(3)
         load_wx(2)
         load_wx(3)
 
@@ -293,30 +293,28 @@ def tile_dualstreamattentionwithrotaryembedding_pa_kernel(
         for b in range(2):
             quantize_tok(b, 0)
         interleave_wc(1)
-        quantize_wc(1)
         prep_gains()
         for pt in range(4):
             for b in range(2):
                 build_tables(b, pt)
+        interleave_wx(0)
+        quantize_wx(0)
+        quantize_wc(1)
+        widen(1)
         interleave_wc(2)
         quantize_wc(2)
+        interleave_wc(3)
         for b in range(2):
             for pt in range(1, 4):
                 turn_tok(b, pt)
-        widen(1)
         interleave_wx(1)
-        interleave_wc(3)
-        widen(2)
-        interleave_wx(2)
-        interleave_wx(0)
-        quantize_wx(0)
+        quantize_wx(1)
+        quantize_wc(3)
         for b in range(2):
             for pt in range(1, 4):
                 quantize_tok(b, pt)
-        quantize_wx(1)
-        quantize_wc(3)
-        quantize_wx(2)
         c_banks = [project("c", C_TILES, j) for j in range(NCH)]
+        widen(2)
         pairs = [(C_TILES, j, c_banks[j]) for j in range(NCH)]
         x_pairs = [(tiles, j) for j in range(NCH) for tiles in X_TILES]
         for i in range(len(pairs) + len(x_pairs)):
@@ -325,8 +323,10 @@ def tile_dualstreamattentionwithrotaryembedding_pa_kernel(
             if i < len(x_pairs):
                 tiles, j = x_pairs[i]
                 pairs.append((tiles, j, project("x", tiles, j)))
-            if i == 1:
-                widen(3)
             if i == 3:
+                interleave_wx(2)
+                quantize_wx(2)
+                widen(3)
+            if i == 5:
                 interleave_wx(3)
                 quantize_wx(3)

@@ -58,17 +58,15 @@ def tile_dualstreamattentionwithrotaryembedding_pa_kernel(
         wx_bytes = {}
         tok = {}
 
-        def load_wc(j):
-            t = stage.tile([P, 2, 4, CH], BF16, name="wc_raw", tag="big")
-            for g in range(2):
-                nc.sync.dma_start(out=t[:, g], in_=wc_view[g][:, :, j * CH : (j + 1) * CH])
-                wc_raw[(j, g)] = t[:, g]
+        def load_wc(j, g):
+            if g == 0:
+                wc_raw[j] = stage.tile([P, 2, 4, CH], BF16, name="wc_raw", tag="big")
+            nc.sync.dma_start(out=wc_raw[j][:, g], in_=wc_view[g][:, :, j * CH : (j + 1) * CH])
 
-        def load_wx(j):
-            for g in range(2):
-                t = keep.tile([P, 4, CH], U8, name="wx_bytes_%d_%d" % (j, g))
-                nc.sync.dma_start(out=t[:], in_=wx_view[g][:, :, j * CH : (j + 1) * CH])
-                wx_bytes[(j, g)] = t
+        def load_wx(j, g):
+            t = keep.tile([P, 4, CH], U8, name="wx_bytes_%d_%d" % (j, g))
+            nc.sync.dma_start(out=t[:], in_=wx_view[g][:, :, j * CH : (j + 1) * CH])
+            wx_bytes[(j, g)] = t
 
         def load_tok(b, pt):
             t = keep.tile([P, D], BF16, name="tok_%d_%d" % (b, pt))
@@ -81,29 +79,39 @@ def tile_dualstreamattentionwithrotaryembedding_pa_kernel(
         wx_scale = keep.tile([P, 2, 8], F32, name="wx_scale")
         fr = keep.tile([P, 8, 64, 2, 1], BF16, name="fr")
 
-        def load_table_inputs():
+        def load_gains():
             for i, vec in enumerate((qn_c, kn_c, qn_x, kn_x)):
                 nc.sync.dma_start(out=grow[0:1, i, :], in_=vec.rearrange("(o d) -> o d", o=1))
+
+        def load_angles():
             nc.sync.dma_start(
                 out=fr[:].rearrange("p f j c o -> p f (j c o)"),
                 in_=freqs_cis.rearrange("b (t p) j c -> p (b t) (j c)", p=P),
             )
 
-        load_wc(0)
+        load_wc(0, 0)
         nc.sync.dma_start(out=wx_scale[:, :, 0:4], in_=Wqk_x_scale.rearrange("(g p t) o -> p g (t o)", p=P, t=4))
-        load_wx(0)
+        load_wx(0, 0)
+        load_gains()
+        load_wc(0, 1)
+        load_wx(0, 1)
+        load_angles()
+        for g in range(2):
+            load_wc(1, g)
         load_tok(0, 0)
         load_tok(1, 0)
-        load_wc(1)
-        load_table_inputs()
-        load_wc(2)
-        load_wx(1)
-        load_wc(3)
+        for g in range(2):
+            load_wc(2, g)
+        for g in range(2):
+            load_wx(1, g)
+        for g in range(2):
+            load_wc(3, g)
         for b in range(2):
             for pt in range(1, 4):
                 load_tok(b, pt)
-        load_wx(2)
-        load_wx(3)
+        for j in (2, 3):
+            for g in range(2):
+                load_wx(j, g)
 
         tokc = {}
         toks = {}
@@ -170,29 +178,27 @@ def tile_dualstreamattentionwithrotaryembedding_pa_kernel(
 
         wide = {}
 
-        def widen(j):
-            for g in range(2):
-                w = stage.tile([P, 4, CH], BF16, name="wide", bufs=6)
-                for t in range(4):
-                    nc.scalar.activation(
-                        out=w[:, t, :],
-                        in_=wx_bytes[(j, g)][:, t, :].bitcast(FP8),
-                        func=ACT.Copy,
-                        scale=wx_scale[:, g, t : t + 1],
-                    )
-                wide[(j, g)] = w[:]
+        def widen(j, g):
+            w = stage.tile([P, 4, CH], BF16, name="wide", bufs=6)
+            for t in range(4):
+                nc.scalar.activation(
+                    out=w[:, t, :],
+                    in_=wx_bytes[(j, g)][:, t, :].bitcast(FP8),
+                    func=ACT.Copy,
+                    scale=wx_scale[:, g, t : t + 1],
+                )
+            wide[(j, g)] = w[:]
 
         def interleave_wc(j):
             for g in range(2):
-                interleave("c", j, g, wc_raw[(j, g)], INTERLEAVER["c"][j])
+                interleave("c", j, g, wc_raw[j][:, g], INTERLEAVER["c"][j])
 
         def quantize_wc(j):
             quantize_w("c", j, 0)
             quantize_w("c", j, 1)
 
-        def interleave_wx(j):
-            for g in range(2):
-                interleave("x", j, g, wide[(j, g)], INTERLEAVER["x"][j])
+        def interleave_wx(j, g):
+            interleave("x", j, g, wide[(j, g)], INTERLEAVER["x"][j])
 
         def quantize_wx(j):
             quantize_w("x", j, 0)
@@ -253,80 +259,121 @@ def tile_dualstreamattentionwithrotaryembedding_pa_kernel(
             nc.scalar.activation(out=rstd[:], in_=ss[:], func=ACT.Abs_reciprocal_sqrt, scale=1.0 / HD, bias=EPS)
             return accs, rstd
 
-        def rotate(accs, rstd, tiles, j, own=False):
+        def rotate(accs, rstd, tiles, j, adder="G", before_last_head=None):
             qk = j // 2
             h0 = 4 * (j % 2)
             uv = stage.tile([P, 8, 2, HD], F32, name="uv", tag="big")
-            for k in range(2):
-                b, pt = tiles[k]
-                for h in range(4):
-                    nc.vector.scalar_tensor_tensor(
-                        out=uv[:, 4 * k + h],
-                        in0=accs[k][:, h * HD : (h + 1) * HD].rearrange("p (o d) -> p o d", o=1).to_broadcast([P, 2, HD]),
-                        scalar=rstd[:, 4 * k + h : 4 * k + h + 1],
-                        in1=tabA[(b, pt, qk)][:].rearrange("p r j e -> p r (j e)"),
-                        op0=ALU.mult,
-                        op1=ALU.mult,
-                    )
             uv5 = uv[:].rearrange("p h r (j e) -> p h r j e", e=2)
             r = stage.tile([P, 8, 64, 2], F32, name="r", bufs=3)
-            if not own:
-                nc.gpsimd.tensor_tensor(out=r[:], in0=uv5[:, :, 0], in1=uv5[:, :, 1, :, ::-1], op=ALU.add)
-            for k in range(2):
+
+            def products(k, h):
+                nc.vector.scalar_tensor_tensor(
+                    out=uv[:, 4 * k + h],
+                    in0=accs[k][:, h * HD : (h + 1) * HD].rearrange("p (o d) -> p o d", o=1).to_broadcast([P, 2, HD]),
+                    scalar=rstd[:, 4 * k + h : 4 * k + h + 1],
+                    in1=tabA[tiles[k] + (qk,)][:].rearrange("p r j e -> p r (j e)"),
+                    op0=ALU.mult,
+                    op1=ALU.mult,
+                )
+
+            def add(engine, hs):
+                engine.tensor_tensor(out=r[:, hs], in0=uv5[:, hs, 0], in1=uv5[:, hs, 1, :, ::-1], op=ALU.add)
+
+            def store(k):
                 b, pt = tiles[k]
-                if own:
-                    hs = slice(4 * k, 4 * k + 4)
-                    nc.vector.tensor_tensor(out=r[:, hs], in0=uv5[:, hs, 0], in1=uv5[:, hs, 1, :, ::-1], op=ALU.add)
                 nc.sync.dma_start(
                     out=outs[qk][b, h0 : h0 + 4, pt * P : (pt + 1) * P, :].rearrange("h p d -> p h d"),
                     in_=r[:, 4 * k : 4 * k + 4].rearrange("p h j e -> p h (j e)"),
                 )
 
+            banks = (slice(0, 4), slice(4, 8))
+            for k in range(2):
+                for h in range(4):
+                    if before_last_head is not None and (k, h) == (1, 3):
+                        before_last_head()
+                    products(k, h)
+                if adder == "V, bank by bank":
+                    add(nc.vector, banks[k])
+                    store(k)
+            if adder == "G":
+                add(nc.gpsimd, slice(0, 8))
+                store(0)
+                store(1)
+            elif adder == "V":
+                for k in range(2):
+                    add(nc.vector, banks[k])
+                    store(k)
+
         C_TILES = ((0, 0), (1, 0))
         X_TILES = (((0, 1), (0, 2)), ((0, 3), (1, 1)), ((1, 2), (1, 3)))
 
-        for b in range(2):
-            turn_tok(b, 0)
-        widen(0)
-        interleave_wc(0)
-        quantize_wc(0)
-        for b in range(2):
-            quantize_tok(b, 0)
-        interleave_wc(1)
-        prep_gains()
-        for pt in range(4):
+        def first_phase():
+            for g in range(2):
+                widen(0, g)
+            interleave_wc(0)
+            quantize_wc(0)
+            prep_gains()
+            interleave_wc(1)
             for b in range(2):
-                build_tables(b, pt)
-        interleave_wx(0)
-        quantize_wx(0)
-        quantize_wc(1)
-        widen(1)
-        interleave_wc(2)
-        quantize_wc(2)
-        interleave_wc(3)
-        for b in range(2):
-            for pt in range(1, 4):
-                turn_tok(b, pt)
-        interleave_wx(1)
-        quantize_wx(1)
-        quantize_wc(3)
-        for b in range(2):
-            for pt in range(1, 4):
-                quantize_tok(b, pt)
-        c_banks = [project("c", C_TILES, j) for j in range(NCH)]
-        widen(2)
-        pairs = [(C_TILES, j, c_banks[j]) for j in range(NCH)]
-        x_pairs = [(tiles, j) for j in range(NCH) for tiles in X_TILES]
-        for i in range(len(pairs) + len(x_pairs)):
-            tiles, j, banks = pairs[i]
-            rotate(*banks, tiles, j, own=(i >= 14))
-            if i < len(x_pairs):
-                tiles, j = x_pairs[i]
-                pairs.append((tiles, j, project("x", tiles, j)))
-            if i == 3:
-                interleave_wx(2)
-                quantize_wx(2)
-                widen(3)
-            if i == 5:
-                interleave_wx(3)
-                quantize_wx(3)
+                build_tables(b, 0)
+            for b in range(2):
+                build_tables(b, 1)
+            for g in range(2):
+                interleave_wx(0, g)
+            quantize_wx(0)
+            for b in range(2):
+                turn_tok(b, 0)
+            quantize_wc(1)
+            for pt in (2, 3):
+                for b in range(2):
+                    build_tables(b, pt)
+            interleave_wc(2)
+            for g in range(2):
+                widen(1, g)
+            for b in range(2):
+                quantize_tok(b, 0)
+            quantize_wc(2)
+            interleave_wc(3)
+            for g in range(2):
+                interleave_wx(1, g)
+            quantize_wx(1)
+            for b in range(2):
+                for pt in range(1, 4):
+                    turn_tok(b, pt)
+            quantize_wc(3)
+            for b in range(2):
+                for pt in range(1, 4):
+                    quantize_tok(b, pt)
+
+        def vector_x2():
+            for g in range(2):
+                interleave_wx(2, g)
+            quantize_wx(2)
+
+        def second_phase():
+            pairs = [(project("c", C_TILES, j), C_TILES, j) for j in range(NCH)]
+            for g in range(2):
+                widen(2, g)
+            ahead = [(tiles, j) for j in range(NCH) for tiles in X_TILES]
+            vector_blocks = {3: vector_x2, 11: lambda: quantize_wx(3)}
+            scalar_blocks = {
+                2: lambda: widen(3, 0),
+                4: lambda: widen(3, 1),
+                7: lambda: interleave_wx(3, 0),
+                8: lambda: interleave_wx(3, 1),
+            }
+            for i in range(4 + len(ahead)):
+                (accs, rstd), tiles, j = pairs[i]
+                adder = {14: "V", 15: "V, bank by bank"}.get(i, "G")
+                rotate(accs, rstd, tiles, j, adder, vector_blocks.get(i))
+                if i in scalar_blocks:
+                    scalar_blocks[i]()
+                while len(pairs) < 4 + len(ahead) and len(pairs) <= i + 4:
+                    tiles, j = ahead[len(pairs) - 4]
+                    if j == 3 and i < 11:
+                        break
+                    pairs.append((project("x", tiles, j), tiles, j))
+
+        with tc.manual_schedule(engines={mybir.EngineType.PE, mybir.EngineType.DVE, mybir.EngineType.Activation}):
+            first_phase()
+            second_phase()

@@ -22,10 +22,9 @@ CH = 512
 NCH = 4
 EPS = 1e-6
 
-INTERLEAVER = {
-    "c": ("V", "T", "T", "T"),
-    "x": ("V", "V", "V", "S"),
-}
+C_TILES = ((0, 0), (1, 0))
+HALVES = ((0, 0), (0, 1), (1, 0), (1, 1))
+X_TILES = (((0, 1), (0, 2)), ((0, 3), (1, 1)), ((1, 2), (1, 3)))
 
 
 def tile_dualstreamattentionwithrotaryembedding_pa_kernel(
@@ -96,22 +95,20 @@ def tile_dualstreamattentionwithrotaryembedding_pa_kernel(
         load_wc(0, 1)
         load_wx(0, 1)
         load_angles()
-        for g in range(2):
-            load_wc(1, g)
         load_tok(0, 0)
         load_tok(1, 0)
-        for g in range(2):
-            load_wc(2, g)
-        for g in range(2):
-            load_wx(1, g)
-        for g in range(2):
-            load_wc(3, g)
+        for j in (1, 2):
+            for g in range(2):
+                load_wc(j, g)
+            for g in range(2):
+                load_wx(j, g)
         for b in range(2):
             for pt in range(1, 4):
                 load_tok(b, pt)
-        for j in (2, 3):
-            for g in range(2):
-                load_wx(j, g)
+        for g in range(2):
+            load_wc(3, g)
+        for g in range(2):
+            load_wx(3, g)
 
         tokc = {}
         toks = {}
@@ -143,30 +140,34 @@ def tile_dualstreamattentionwithrotaryembedding_pa_kernel(
 
         grouped_w = {}
 
-        def interleave(stream, j, g, src, eng):
-            grouped = stage.tile([P, 4 * CH], BF16, name="wg_" + eng, align_bytes=64)
-            o = grouped[:].rearrange("p (c i t) -> p c t i", i=4, t=4)
-            i = src.rearrange("p t (c i) -> p c t i", i=4)
-            if eng == "V":
-                nc.vector.tensor_copy(out=o, in_=i)
-            elif eng == "S":
-                nc.scalar.copy(out=o, in_=i)
-            else:
-                for h in range(2):
-                    bank = psum.tile([P, 2, 4 * P], BF16, name="turned", tag="bank")
-                    for q in range(2):
-                        cols = slice((2 * h + q) * P, (2 * h + q + 1) * P)
-                        nc.tensor.matmul(
-                            out=bank[:, q].rearrange("p (n t) -> p t n", t=4),
-                            lhsT=ident_b[:],
-                            rhs=src[:, :, cols],
-                            start=True,
-                            stop=True,
-                        )
-                    nc.scalar.copy(
-                        out=grouped[:, h * 2 * CH : (h + 1) * 2 * CH], in_=bank[:].rearrange("p q m -> p (q m)")
-                    )
+        def interleave(engine_copy, tag, stream, j, g, source):
+            grouped = stage.tile([P, 4 * CH], BF16, name=tag, align_bytes=64)
+            engine_copy(
+                out=grouped[:].rearrange("p (c i t) -> p c t i", i=4, t=4),
+                in_=source.rearrange("p t (c i) -> p c t i", i=4),
+            )
             grouped_w[(stream, j, g)] = grouped
+
+        def turn_half(j, g, h):
+            bank = psum.tile([P, 2, 4 * P], BF16, name="turned", tag="bank")
+            for q in range(2):
+                cols = slice((2 * h + q) * P, (2 * h + q + 1) * P)
+                nc.tensor.matmul(
+                    out=bank[:, q].rearrange("p (n t) -> p t n", t=4),
+                    lhsT=ident_b[:],
+                    rhs=wc_raw[j][:, g, :, cols],
+                    start=True,
+                    stop=True,
+                )
+            return bank
+
+        def empty_half(j, g, h, bank):
+            if h == 0:
+                grouped_w[("c", j, g)] = stage.tile([P, 4 * CH], BF16, name="wg_T", align_bytes=64)
+            nc.scalar.copy(
+                out=grouped_w[("c", j, g)][:, h * 2 * CH : (h + 1) * 2 * CH],
+                in_=bank[:].rearrange("p q m -> p (q m)"),
+            )
 
         def quantize_w(stream, j, g):
             grouped = grouped_w[(stream, j, g)]
@@ -178,31 +179,26 @@ def tile_dualstreamattentionwithrotaryembedding_pa_kernel(
 
         wide = {}
 
-        def widen(j, g):
-            w = stage.tile([P, 4, CH], BF16, name="wide", bufs=6)
-            for t in range(4):
+        def widen(j, g, rows):
+            if 0 in rows:
+                wide[(j, g)] = stage.tile([P, 4, CH], BF16, name="wide", bufs=6)
+            for t in rows:
                 nc.scalar.activation(
-                    out=w[:, t, :],
+                    out=wide[(j, g)][:, t, :],
                     in_=wx_bytes[(j, g)][:, t, :].bitcast(FP8),
                     func=ACT.Copy,
                     scale=wx_scale[:, g, t : t + 1],
                 )
-            wide[(j, g)] = w[:]
 
-        def interleave_wc(j):
-            for g in range(2):
-                interleave("c", j, g, wc_raw[j][:, g], INTERLEAVER["c"][j])
+        def turn_beside_widening(j, halves):
+            for g, h in halves:
+                bank = turn_half(j, g, h)
+                widen(j, g, (2 * h, 2 * h + 1))
+                empty_half(j, g, h, bank)
 
-        def quantize_wc(j):
-            quantize_w("c", j, 0)
-            quantize_w("c", j, 1)
-
-        def interleave_wx(j, g):
-            interleave("x", j, g, wide[(j, g)], INTERLEAVER["x"][j])
-
-        def quantize_wx(j):
-            quantize_w("x", j, 0)
-            quantize_w("x", j, 1)
+        def quantize(stream, j):
+            quantize_w(stream, j, 0)
+            quantize_w(stream, j, 1)
 
         g2 = keep.tile([P, 4, 2, 64, 2], BF16, name="g2")
 
@@ -304,76 +300,70 @@ def tile_dualstreamattentionwithrotaryembedding_pa_kernel(
                     add(nc.vector, banks[k])
                     store(k)
 
-        C_TILES = ((0, 0), (1, 0))
-        X_TILES = (((0, 1), (0, 2)), ((0, 3), (1, 1)), ((1, 2), (1, 3)))
-
-        def first_phase():
+        def prepare():
             for g in range(2):
-                widen(0, g)
-            interleave_wc(0)
-            quantize_wc(0)
+                widen(0, g, range(4))
+            for g in range(2):
+                interleave(nc.vector.tensor_copy, "wg_V", "c", 0, g, wc_raw[0][:, g])
+            quantize("c", 0)
             prep_gains()
-            interleave_wc(1)
-            for b in range(2):
-                build_tables(b, 0)
-            for b in range(2):
-                build_tables(b, 1)
-            for g in range(2):
-                interleave_wx(0, g)
-            quantize_wx(0)
+            for pt in (0, 1):
+                for b in range(2):
+                    build_tables(b, pt)
             for b in range(2):
                 turn_tok(b, 0)
-            quantize_wc(1)
+            turn_beside_widening(1, HALVES)
+            for b in range(2):
+                quantize_tok(b, 0)
+            for g in range(2):
+                interleave(nc.vector.tensor_copy, "wg_V", "x", 0, g, wide[(0, g)][:])
+            quantize("x", 0)
             for pt in (2, 3):
                 for b in range(2):
                     build_tables(b, pt)
-            interleave_wc(2)
+            quantize("c", 1)
+            banks = [project("c", C_TILES, 0)]
             for g in range(2):
-                widen(1, g)
-            for b in range(2):
-                quantize_tok(b, 0)
-            quantize_wc(2)
-            interleave_wc(3)
-            for g in range(2):
-                interleave_wx(1, g)
-            quantize_wx(1)
+                interleave(nc.vector.tensor_copy, "wg_V", "x", 1, g, wide[(1, g)][:])
+            quantize("x", 1)
+            turn_beside_widening(2, HALVES)
             for b in range(2):
                 for pt in range(1, 4):
                     turn_tok(b, pt)
-            quantize_wc(3)
+            for g in range(2):
+                interleave(nc.vector.tensor_copy, "wg_V", "x", 2, g, wide[(2, g)][:])
+            quantize("x", 2)
+            quantize("c", 2)
             for b in range(2):
                 for pt in range(1, 4):
                     quantize_tok(b, pt)
+            return banks
 
-        def vector_x2():
-            for g in range(2):
-                interleave_wx(2, g)
-            quantize_wx(2)
+        def rotate_all(banks):
+            pairs = [("c", C_TILES, j) for j in range(3)]
+            pairs += [("x", tiles, 0) for tiles in X_TILES]
+            pairs += [("c", C_TILES, 3)]
+            pairs += [("x", tiles, j) for j in (1, 2, 3) for tiles in X_TILES]
+            n = len(pairs)
 
-        def second_phase():
-            pairs = [(project("c", C_TILES, j), C_TILES, j) for j in range(NCH)]
-            for g in range(2):
-                widen(2, g)
-            ahead = [(tiles, j) for j in range(NCH) for tiles in X_TILES]
-            vector_blocks = {3: vector_x2, 11: lambda: quantize_wx(3)}
-            scalar_blocks = {
-                2: lambda: widen(3, 0),
-                4: lambda: widen(3, 1),
-                7: lambda: interleave_wx(3, 0),
-                8: lambda: interleave_wx(3, 1),
-            }
-            for i in range(4 + len(ahead)):
-                (accs, rstd), tiles, j = pairs[i]
-                adder = {14: "V", 15: "V, bank by bank"}.get(i, "G")
-                rotate(accs, rstd, tiles, j, adder, vector_blocks.get(i))
-                if i in scalar_blocks:
-                    scalar_blocks[i]()
-                while len(pairs) < 4 + len(ahead) and len(pairs) <= i + 4:
-                    tiles, j = ahead[len(pairs) - 4]
-                    if j == 3 and i < 11:
-                        break
-                    pairs.append((project("x", tiles, j), tiles, j))
+            def fill(upto):
+                while len(banks) < min(upto, n):
+                    banks.append(project(*pairs[len(banks)]))
+
+            blocks = {3: ("c", 3), 11: ("x", 3)}
+            fill(3)
+            for i in range(n):
+                stream, tiles, j = pairs[i]
+                if i in (1, 2):
+                    turn_beside_widening(3, HALVES[2 * i - 2 : 2 * i])
+                    fill(3 + i)
+                adder = "G" if i < n - 2 else "V" if i == n - 2 else "V, bank by bank"
+                block = blocks.get(i)
+                rotate(*banks[i], tiles, j, adder, None if block is None else (lambda: quantize(*block)))
+                if i in (7, 8):
+                    interleave(nc.scalar.copy, "wg_S", "x", 3, i - 7, wide[(3, i - 7)][:])
+                if i >= 2:
+                    fill(min(i + 4, 6 if i == 2 else 13 if i < 11 else n))
 
         with tc.manual_schedule(engines={mybir.EngineType.PE, mybir.EngineType.DVE, mybir.EngineType.Activation}):
-            first_phase()
-            second_phase()
+            rotate_all(prepare())

@@ -88,13 +88,13 @@ def tile_dualstreamattentionwithrotaryembedding_pa_kernel(
                 in_=freqs_cis.rearrange("b (t p) j c -> p (b t) (j c)", p=P),
             )
 
-        load_wc(0, 0)
         nc.sync.dma_start(out=wx_scale[:, :, 0:4], in_=Wqk_x_scale.rearrange("(g p t) o -> p g (t o)", p=P, t=4))
         load_wx(0, 0)
-        load_gains()
-        load_wc(0, 1)
         load_wx(0, 1)
+        load_wc(0, 0)
+        load_gains()
         load_angles()
+        load_wc(0, 1)
         load_tok(0, 0)
         load_tok(1, 0)
         for j in (1, 2):
@@ -124,6 +124,9 @@ def tile_dualstreamattentionwithrotaryembedding_pa_kernel(
             for g in range(2):
                 for u in range(2):
                     nc.tensor.transpose(xt[:, 2 * g + u, :], words[:, 256 * g + u : 256 * (g + 1) : 2], ident[:])
+            return xt
+
+        def empty_tok(b, pt, xt):
             grouped = stage.tile([P, D], BF16, name="tokg", bufs=6, align_bytes=64)
             nc.scalar.copy(
                 out=grouped[:].bitcast(F32).rearrange("p (g r u) -> p g r u", g=2, u=2),
@@ -140,8 +143,8 @@ def tile_dualstreamattentionwithrotaryembedding_pa_kernel(
 
         grouped_w = {}
 
-        def interleave(engine_copy, tag, stream, j, g, source):
-            grouped = stage.tile([P, 4 * CH], BF16, name=tag, align_bytes=64)
+        def interleave(engine_copy, tag, bufs, stream, j, g, source):
+            grouped = stage.tile([P, 4 * CH], BF16, name=tag, bufs=bufs, align_bytes=64)
             engine_copy(
                 out=grouped[:].rearrange("p (c i t) -> p c t i", i=4, t=4),
                 in_=source.rearrange("p t (c i) -> p c t i", i=4),
@@ -179,22 +182,24 @@ def tile_dualstreamattentionwithrotaryembedding_pa_kernel(
 
         wide = {}
 
-        def widen(j, g, rows):
+        def widen(j, g, rows, on_vector=False):
             if 0 in rows:
                 wide[(j, g)] = stage.tile([P, 4, CH], BF16, name="wide", bufs=6)
             for t in rows:
-                nc.scalar.activation(
-                    out=wide[(j, g)][:, t, :],
-                    in_=wx_bytes[(j, g)][:, t, :].bitcast(FP8),
-                    func=ACT.Copy,
-                    scale=wx_scale[:, g, t : t + 1],
-                )
+                out = wide[(j, g)][:, t, :]
+                row = wx_bytes[(j, g)][:, t, :].bitcast(FP8)
+                scale = wx_scale[:, g, t : t + 1]
+                if on_vector:
+                    nc.vector.tensor_scalar(out=out, in0=row, scalar1=scale, scalar2=None, op0=ALU.mult)
+                else:
+                    nc.scalar.activation(out=out, in_=row, func=ACT.Copy, scale=scale)
 
-        def turn_beside_widening(j, halves):
-            for g, h in halves:
-                bank = turn_half(j, g, h)
-                widen(j, g, (2 * h, 2 * h + 1))
-                empty_half(j, g, h, bank)
+        def turn_halves(j, halves):
+            return [(j, g, h, turn_half(j, g, h)) for g, h in halves]
+
+        def empty_halves(turned):
+            for item in turned:
+                empty_half(*item)
 
         def quantize(stream, j):
             quantize_w(stream, j, 0)
@@ -260,7 +265,7 @@ def tile_dualstreamattentionwithrotaryembedding_pa_kernel(
             h0 = 4 * (j % 2)
             uv = stage.tile([P, 8, 2, HD], F32, name="uv", tag="big")
             uv5 = uv[:].rearrange("p h r (j e) -> p h r j e", e=2)
-            r = stage.tile([P, 8, 64, 2], F32, name="r", bufs=3)
+            r = stage.tile([P, 8, 64, 2], F32, name="r", bufs=4)
 
             def products(k, h):
                 nc.vector.scalar_tensor_tensor(
@@ -300,70 +305,82 @@ def tile_dualstreamattentionwithrotaryembedding_pa_kernel(
                     add(nc.vector, banks[k])
                     store(k)
 
+        X_TOKENS = [(b, pt) for b in range(2) for pt in range(1, 4)]
+
+        def interleave_on_vector(stream, j, source):
+            for g in range(2):
+                interleave(nc.vector.tensor_copy, "wg_V", 4, stream, j, g, source(g))
+
         def prepare():
             for g in range(2):
-                widen(0, g, range(4))
-            for g in range(2):
-                interleave(nc.vector.tensor_copy, "wg_V", "c", 0, g, wc_raw[0][:, g])
-            quantize("c", 0)
+                widen(0, g, range(4), on_vector=True)
             prep_gains()
+            for g in range(2):
+                interleave(nc.scalar.copy, "wg_S", 2, "x", 0, g, wide[(0, g)][:])
             for pt in (0, 1):
                 for b in range(2):
                     build_tables(b, pt)
+            turned = turn_halves(0, HALVES[:2])
+            c_banks = [turn_tok(*tile) for tile in C_TILES]
+            turned += turn_halves(0, HALVES[2:])
+            for tile, bank in zip(C_TILES, c_banks):
+                empty_tok(*tile, bank)
+            empty_halves(turned)
             for b in range(2):
-                turn_tok(b, 0)
-            turn_beside_widening(1, HALVES)
-            for b in range(2):
-                quantize_tok(b, 0)
-            for g in range(2):
-                interleave(nc.vector.tensor_copy, "wg_V", "x", 0, g, wide[(0, g)][:])
+                build_tables(b, 2)
             quantize("x", 0)
-            for pt in (2, 3):
-                for b in range(2):
-                    build_tables(b, pt)
+            for tile in C_TILES:
+                quantize_tok(*tile)
+            for b in range(2):
+                build_tables(b, 3)
+            quantize("c", 0)
+            for g in range(2):
+                widen(1, g, range(4))
+            interleave_on_vector("c", 1, lambda g: wc_raw[1][:, g])
             quantize("c", 1)
+            empty_halves(turn_halves(2, HALVES))
             banks = [project("c", C_TILES, 0)]
-            for g in range(2):
-                interleave(nc.vector.tensor_copy, "wg_V", "x", 1, g, wide[(1, g)][:])
+            interleave_on_vector("x", 1, lambda g: wide[(1, g)][:])
             quantize("x", 1)
-            turn_beside_widening(2, HALVES)
-            for b in range(2):
-                for pt in range(1, 4):
-                    turn_tok(b, pt)
-            for g in range(2):
-                interleave(nc.vector.tensor_copy, "wg_V", "x", 2, g, wide[(2, g)][:])
-            quantize("x", 2)
+            for tile in X_TOKENS:
+                empty_tok(*tile, turn_tok(*tile))
             quantize("c", 2)
-            for b in range(2):
-                for pt in range(1, 4):
-                    quantize_tok(b, pt)
+            for g in range(2):
+                widen(2, g, range(4), on_vector=True)
+            interleave_on_vector("x", 2, lambda g: wide[(2, g)][:])
+            quantize("x", 2)
+            for tile in X_TOKENS:
+                quantize_tok(*tile)
+            for j in (1, 2):
+                banks.append(project("c", C_TILES, j))
+            empty_halves(turn_halves(3, HALVES[:2]))
+            widen(3, 0, (0, 1))
             return banks
 
         def rotate_all(banks):
             pairs = [("c", C_TILES, j) for j in range(3)]
-            pairs += [("x", tiles, 0) for tiles in X_TILES]
+            pairs += [("x", tiles, j) for j in (0, 1) for tiles in X_TILES]
             pairs += [("c", C_TILES, 3)]
-            pairs += [("x", tiles, j) for j in (1, 2, 3) for tiles in X_TILES]
+            pairs += [("x", tiles, j) for j in (2, 3) for tiles in X_TILES]
             n = len(pairs)
-
-            def fill(upto):
-                while len(banks) < min(upto, n):
-                    banks.append(project(*pairs[len(banks)]))
-
-            blocks = {3: ("c", 3), 11: ("x", 3)}
-            fill(3)
+            blocks = {3: lambda: quantize("c", 3), 10: lambda: quantize("x", 3)}
+            steps = {
+                1: lambda: empty_halves(turn_halves(3, HALVES[2:])),
+                2: lambda: widen(3, 0, (2, 3)),
+                3: lambda: widen(3, 1, (0, 1)),
+                4: lambda: widen(3, 1, (2, 3)),
+                5: lambda: interleave(nc.scalar.copy, "wg_S", 2, "x", 3, 0, wide[(3, 0)][:]),
+                7: lambda: interleave(nc.scalar.copy, "wg_S", 2, "x", 3, 1, wide[(3, 1)][:]),
+            }
             for i in range(n):
                 stream, tiles, j = pairs[i]
-                if i in (1, 2):
-                    turn_beside_widening(3, HALVES[2 * i - 2 : 2 * i])
-                    fill(3 + i)
                 adder = "G" if i < n - 2 else "V" if i == n - 2 else "V, bank by bank"
-                block = blocks.get(i)
-                rotate(*banks[i], tiles, j, adder, None if block is None else (lambda: quantize(*block)))
-                if i in (7, 8):
-                    interleave(nc.scalar.copy, "wg_S", "x", 3, i - 7, wide[(3, i - 7)][:])
-                if i >= 2:
-                    fill(min(i + 4, 6 if i == 2 else 13 if i < 11 else n))
+                rotate(*banks[i], tiles, j, adder, blocks.get(i))
+                if i in steps:
+                    steps[i]()
+                ready = n if i >= 10 else n - 3
+                while len(banks) < min(i + 5, ready):
+                    banks.append(project(*pairs[len(banks)]))
 
         with tc.manual_schedule(engines={mybir.EngineType.PE, mybir.EngineType.DVE, mybir.EngineType.Activation}):
             rotate_all(prepare())

from contextlib import ExitStack

import concourse.mybir as mybir
from concourse.masks import make_identity

FLOPS = 2 * 1024 * 1024 * 2048

F32 = mybir.dt.float32
BF16 = mybir.dt.bfloat16
U32 = mybir.dt.uint32
I32 = mybir.dt.int32
U8 = mybir.dt.uint8
FP8 = mybir.dt.float8_e4m3fn
FP8X4 = mybir.dt.float8_e4m3fn_x4
ACT = mybir.ActivationFunctionType
ALU = mybir.AluOpType

P = 128
D = 1024
HD = 128
CH = 512
NCH = 4
EPS = 1e-6

C_TILES = ((0, 0), (1, 0))
HALVES = ((0, 0), (0, 1), (1, 0), (1, 1))
X_TILES = (((0, 1), (0, 2)), ((0, 3), (1, 1)), ((1, 2), (1, 3)))


def tile_dualstreamattentionwithrotaryembedding_pa_kernel(
    tc, x, c, freqs_cis, Wqk_x_bytes, Wqk_x_scale, qn_x, kn_x, Wqk_c, qn_c, kn_c, out_0, out_1
):
    nc = tc.nc
    outs = (out_0, out_1)
    with ExitStack() as ctx:
        keep = ctx.enter_context(tc.tile_pool(name="keep", bufs=1))
        stage = ctx.enter_context(tc.tile_pool(name="stage", bufs=4))
        small = ctx.enter_context(tc.tile_pool(name="small", bufs=8))
        psum = ctx.enter_context(tc.psum_pool(name="psum", bufs=8))

        grow = keep.tile([P, 4, HD], BF16, name="grow")
        nc.vector.memset(grow[:].rearrange("p i d -> p (i d)").bitcast(I32), 0)
        ones_b = keep.tile([P, P], BF16, name="ones_b")
        nc.gpsimd.memset(ones_b[:], 1.0)
        ident = keep.tile([P, P], F32, name="ident")
        make_identity(nc, ident[:])
        ident_b = keep.tile([P, P], BF16, name="ident_b")
        make_identity(nc, ident_b[:])
        one = keep.tile([P, 1], F32, name="one")
        nc.vector.memset(one[:], 1.0)
        warm = keep.tile([P, 1], F32, name="warm")
        nc.scalar.activation(out=warm[:], in_=one[:], func=ACT.Abs_reciprocal_sqrt)

        wc_view = Wqk_c.rearrange("(g p t) n -> g p t n", p=P, t=4)
        wx_view = Wqk_x_bytes.rearrange("(g p t) n -> g p t n", p=P, t=4)
        wc_raw = {}
        wx_bytes = {}
        tok = {}

        def load_wc(j, g):
            if g == 0:
                wc_raw[j] = stage.tile([P, 2, 4, CH], BF16, name="wc_raw", tag="big")
            nc.sync.dma_start(out=wc_raw[j][:, g], in_=wc_view[g][:, :, j * CH : (j + 1) * CH])

        def load_wx(j, g):
            t = keep.tile([P, 4, CH], U8, name="wx_bytes_%d_%d" % (j, g))
            nc.sync.dma_start(out=t[:], in_=wx_view[g][:, :, j * CH : (j + 1) * CH])
            wx_bytes[(j, g)] = t

        def load_tok(b, pt):
            t = keep.tile([P, D], BF16, name="tok_%d_%d" % (b, pt))
            if pt == 0:
                nc.sync.dma_start(out=t[:], in_=c[b])
            else:
                nc.sync.dma_start(out=t[:], in_=x[b, (pt - 1) * P : pt * P, :])
            tok[(b, pt)] = t

        wx_scale = keep.tile([P, 2, 8], F32, name="wx_scale")
        fr = keep.tile([P, 8, 64, 2, 1], BF16, name="fr")

        def load_gains():
            for i, vec in enumerate((qn_c, kn_c, qn_x, kn_x)):
                nc.sync.dma_start(out=grow[0:1, i, :], in_=vec.rearrange("(o d) -> o d", o=1))

        def load_angles():
            nc.sync.dma_start(
                out=fr[:].rearrange("p f j c o -> p f (j c o)"),
                in_=freqs_cis.rearrange("b (t p) j c -> p (b t) (j c)", p=P),
            )

        nc.sync.dma_start(out=wx_scale[:, :, 0:4], in_=Wqk_x_scale.rearrange("(g p t) o -> p g (t o)", p=P, t=4))
        load_wx(0, 0)
        load_wx(0, 1)
        load_wc(0, 0)
        load_gains()
        load_angles()
        load_wc(0, 1)
        load_tok(0, 0)
        load_tok(1, 0)
        for j in (1, 2):
            for g in range(2):
                load_wc(j, g)
            for g in range(2):
                load_wx(j, g)
        for b in range(2):
            for pt in range(1, 4):
                load_tok(b, pt)
        for g in range(2):
            load_wc(3, g)
        for g in range(2):
            load_wx(3, g)

        tokc = {}
        toks = {}
        wcodes = {}
        wscales = {}
        tabA = {}

        tok_grouped = {}

        def turn_tok(b, pt):
            words = tok[(b, pt)][:].bitcast(F32)
            xt = psum.tile([P, 4, P], F32, name="xt", tag="bank")
            for g in range(2):
                for u in range(2):
                    nc.tensor.transpose(xt[:, 2 * g + u, :], words[:, 256 * g + u : 256 * (g + 1) : 2], ident[:])
            return xt

        def empty_tok(b, pt, xt):
            grouped = stage.tile([P, D], BF16, name="tokg", bufs=6, align_bytes=64)
            nc.scalar.copy(
                out=grouped[:].bitcast(F32).rearrange("p (g r u) -> p g r u", g=2, u=2),
                in_=xt[:].rearrange("p (g u) r -> p g r u", g=2),
            )
            tok_grouped[(b, pt)] = grouped

        def quantize_tok(b, pt):
            codes = keep.tile([P, 2 * P], U32, name="tokc_%d_%d" % (b, pt), align_bytes=64)
            scl = keep.tile([P, 2 * P], U8, name="toks_%d_%d" % (b, pt), align_bytes=64)
            nc.vector.quantize_mx(out=codes[:].bitcast(FP8X4), scales=scl[:], in_=tok_grouped[(b, pt)][:])
            tokc[(b, pt)] = codes
            toks[(b, pt)] = scl

        grouped_w = {}

        def interleave(engine_copy, tag, bufs, stream, j, g, source):
            grouped = stage.tile([P, 4 * CH], BF16, name=tag, bufs=bufs, align_bytes=64)
            engine_copy(
                out=grouped[:].rearrange("p (c i t) -> p c t i", i=4, t=4),
                in_=source.rearrange("p t (c i) -> p c t i", i=4),
            )
            grouped_w[(stream, j, g)] = grouped

        def turn_half(j, g, h):
            bank = psum.tile([P, 2, 4 * P], BF16, name="turned", tag="bank")
            for q in range(2):
                cols = slice((2 * h + q) * P, (2 * h + q + 1) * P)
                nc.tensor.matmul(
                    out=bank[:, q].rearrange("p (n t) -> p t n", t=4),
                    lhsT=ident_b[:],
                    rhs=wc_raw[j][:, g, :, cols],
                    start=True,
                    stop=True,
                )
            return bank

        def empty_half(j, g, h, bank):
            if h == 0:
                grouped_w[("c", j, g)] = stage.tile([P, 4 * CH], BF16, name="wg_T", align_bytes=64)
            nc.scalar.copy(
                out=grouped_w[("c", j, g)][:, h * 2 * CH : (h + 1) * 2 * CH],
                in_=bank[:].rearrange("p q m -> p (q m)"),
            )

        def quantize_w(stream, j, g):
            grouped = grouped_w[(stream, j, g)]
            codes = keep.tile([P, CH], U32, name="wcod_%s_%d_%d" % (stream, j, g), align_bytes=64)
            scl = keep.tile([P, CH], U8, name="wscl_%s_%d_%d" % (stream, j, g), align_bytes=64)
            nc.vector.quantize_mx(out=codes[:].bitcast(FP8X4), scales=scl[:], in_=grouped[:])
            wcodes[(stream, j, g)] = codes
            wscales[(stream, j, g)] = scl

        wide = {}

        def widen(j, g, rows, on_vector=False):
            if 0 in rows:
                wide[(j, g)] = stage.tile([P, 4, CH], BF16, name="wide", bufs=6)
            for t in rows:
                out = wide[(j, g)][:, t, :]
                row = wx_bytes[(j, g)][:, t, :].bitcast(FP8)
                scale = wx_scale[:, g, t : t + 1]
                if on_vector:
                    nc.vector.tensor_scalar(out=out, in0=row, scalar1=scale, scalar2=None, op0=ALU.mult)
                else:
                    nc.scalar.activation(out=out, in_=row, func=ACT.Copy, scale=scale)

        def turn_halves(j, halves):
            return [(j, g, h, turn_half(j, g, h)) for g, h in halves]

        def empty_halves(turned):
            for item in turned:
                empty_half(*item)

        def quantize(stream, j):
            quantize_w(stream, j, 0)
            quantize_w(stream, j, 1)

        g2 = keep.tile([P, 4, 2, 64, 2], BF16, name="g2")

        def prep_gains():
            spread = psum.tile([P, 4, 64, 2], BF16, name="spread", tag="bank")
            nc.tensor.matmul(
                out=spread[:].rearrange("p i j e -> p (i j e)"),
                lhsT=ones_b[:],
                rhs=grow[:].rearrange("p i d -> p (i d)"),
                start=True,
                stop=True,
            )
            nc.vector.tensor_copy(out=g2[:, :, 0], in_=spread[:])
            nc.vector.tensor_copy(out=g2[:, :, 1, :, 0], in_=spread[:, :, :, 0])
            nc.vector.tensor_scalar(
                out=g2[:, :, 1, :, 1], in0=spread[:, :, :, 1], scalar1=-1.0, scalar2=None, op0=ALU.mult
            )

        def build_tables(b, pt):
            ft = 4 * b + pt
            s = 0 if pt == 0 else 1
            cs = fr[:, ft].rearrange("p j c o -> p c j o").to_broadcast([P, 2, 64, 2])
            for qk in range(2):
                ta = keep.tile([P, 2, 64, 2], F32, name="tab_%d_%d" % (ft, qk))
                nc.vector.tensor_tensor(out=ta[:], in0=g2[:, 2 * s + qk], in1=cs, op=ALU.mult)
                tabA[(b, pt, qk)] = ta

        def project(stream, tiles, j):
            accs = []
            for b, pt in tiles:
                acc = psum.tile([P, CH], F32, name="acc", tag="bank")
                for g in range(2):
                    nc.tensor.matmul_mx(
                        out=acc[:],
                        lhsT=tokc[(b, pt)][:, g * P : (g + 1) * P].bitcast(FP8X4),
                        lhsT_scale=toks[(b, pt)][:, g * P : (g + 1) * P],
                        rhs=wcodes[(stream, j, g)][:].bitcast(FP8X4),
                        rhs_scale=wscales[(stream, j, g)][:],
                        start=(g == 0),
                        stop=(g == 1),
                    )
                accs.append(acc)
            ss = small.tile([P, 8], F32, name="ss")
            for k in range(2):
                for h in range(4):
                    junk = stage.tile([P, HD], BF16, name="junk")
                    nc.scalar.activation(
                        out=junk[:],
                        in_=accs[k][:, h * HD : (h + 1) * HD],
                        func=ACT.Square,
                        accum_out=ss[:, 4 * k + h : 4 * k + h + 1],
                    )
            rstd = small.tile([P, 8], F32, name="rstd")
            nc.scalar.activation(out=rstd[:], in_=ss[:], func=ACT.Abs_reciprocal_sqrt, scale=1.0 / HD, bias=EPS)
            return accs, rstd

        def rotate(accs, rstd, tiles, j, adder="G", before_last_head=None):
            qk = j // 2
            h0 = 4 * (j % 2)
            uv = stage.tile([P, 8, 2, HD], F32, name="uv", tag="big")
            uv5 = uv[:].rearrange("p h r (j e) -> p h r j e", e=2)
            r = stage.tile([P, 8, 64, 2], F32, name="r", bufs=4)

            def products(k, h):
                nc.vector.scalar_tensor_tensor(
                    out=uv[:, 4 * k + h],
                    in0=accs[k][:, h * HD : (h + 1) * HD].rearrange("p (o d) -> p o d", o=1).to_broadcast([P, 2, HD]),
                    scalar=rstd[:, 4 * k + h : 4 * k + h + 1],
                    in1=tabA[tiles[k] + (qk,)][:].rearrange("p r j e -> p r (j e)"),
                    op0=ALU.mult,
                    op1=ALU.mult,
                )

            def add(engine, hs):
                engine.tensor_tensor(out=r[:, hs], in0=uv5[:, hs, 0], in1=uv5[:, hs, 1, :, ::-1], op=ALU.add)

            def store(k):
                b, pt = tiles[k]
                nc.sync.dma_start(
                    out=outs[qk][b, h0 : h0 + 4, pt * P : (pt + 1) * P, :].rearrange("h p d -> p h d"),
                    in_=r[:, 4 * k : 4 * k + 4].rearrange("p h j e -> p h (j e)"),
                )

            banks = (slice(0, 4), slice(4, 8))
            for k in range(2):
                for h in range(4):
                    if before_last_head is not None and (k, h) == (1, 3):
                        before_last_head()
                    products(k, h)
                if adder == "V, bank by bank":
                    add(nc.vector, banks[k])
                    store(k)
            if adder == "G":
                add(nc.gpsimd, slice(0, 8))
                store(0)
                store(1)
            elif adder == "V":
                for k in range(2):
                    add(nc.vector, banks[k])
                    store(k)

        X_TOKENS = [(b, pt) for b in range(2) for pt in range(1, 4)]

        def interleave_on_vector(stream, j, source):
            for g in range(2):
                interleave(nc.vector.tensor_copy, "wg_V", 4, stream, j, g, source(g))

        def prepare():
            for g in range(2):
                widen(0, g, range(4), on_vector=True)
            prep_gains()
            for g in range(2):
                interleave(nc.scalar.copy, "wg_S", 2, "x", 0, g, wide[(0, g)][:])
            for pt in (0, 1):
                for b in range(2):
                    build_tables(b, pt)
            turned = turn_halves(0, HALVES[:2])
            c_banks = [turn_tok(*tile) for tile in C_TILES]
            turned += turn_halves(0, HALVES[2:])
            for tile, bank in zip(C_TILES, c_banks):
                empty_tok(*tile, bank)
            empty_halves(turned)
            for b in range(2):
                build_tables(b, 2)
            quantize("x", 0)
            for tile in C_TILES:
                quantize_tok(*tile)
            for b in range(2):
                build_tables(b, 3)
            quantize("c", 0)
            for g in range(2):
                widen(1, g, range(4))
            interleave_on_vector("c", 1, lambda g: wc_raw[1][:, g])
            quantize("c", 1)
            empty_halves(turn_halves(2, HALVES))
            banks = [project("c", C_TILES, 0)]
            interleave_on_vector("x", 1, lambda g: wide[(1, g)][:])
            quantize("x", 1)
            for tile in X_TOKENS:
                empty_tok(*tile, turn_tok(*tile))
            quantize("c", 2)
            for g in range(2):
                widen(2, g, range(4), on_vector=True)
            interleave_on_vector("x", 2, lambda g: wide[(2, g)][:])
            quantize("x", 2)
            for tile in X_TOKENS:
                quantize_tok(*tile)
            for j in (1, 2):
                banks.append(project("c", C_TILES, j))
            empty_halves(turn_halves(3, HALVES[:2]))
            widen(3, 0, (0, 1))
            return banks

        def rotate_all(banks):
            pairs = [("c", C_TILES, j) for j in range(3)]
            pairs += [("x", tiles, j) for j in (0, 1) for tiles in X_TILES]
            pairs += [("c", C_TILES, 3)]
            pairs += [("x", tiles, j) for j in (2, 3) for tiles in X_TILES]
            n = len(pairs)
            blocks = {3: lambda: quantize("c", 3), 10: lambda: quantize("x", 3)}
            steps = {
                1: lambda: empty_halves(turn_halves(3, HALVES[2:])),
                2: lambda: widen(3, 0, (2, 3)),
                3: lambda: widen(3, 1, (0, 1)),
                4: lambda: widen(3, 1, (2, 3)),
                5: lambda: interleave(nc.scalar.copy, "wg_S", 2, "x", 3, 0, wide[(3, 0)][:]),
                7: lambda: interleave(nc.scalar.copy, "wg_S", 2, "x", 3, 1, wide[(3, 1)][:]),
            }
            for i in range(n):
                stream, tiles, j = pairs[i]
                adder = "G" if i < n - 2 else "V" if i == n - 2 else "V, bank by bank"
                rotate(*banks[i], tiles, j, adder, blocks.get(i))
                if i in steps:
                    steps[i]()
                ready = n if i >= 10 else n - 3
                while len(banks) < min(i + 5, ready):
                    banks.append(project(*pairs[len(banks)]))

        with tc.manual_schedule(engines={mybir.EngineType.PE, mybir.EngineType.DVE, mybir.EngineType.Activation}):
            rotate_all(prepare())
